import numpy as np
import ml_dtypes


def mxq(x, axis, fmt="e4m3"):
    dtype, down = {"e4m3": (ml_dtypes.float8_e4m3fn, 7), "e5m2": (ml_dtypes.float8_e5m2, 14)}[fmt]
    v = np.moveaxis(np.asarray(x, np.float32).astype(ml_dtypes.bfloat16).astype(np.float64), axis, -1)
    blocks = v.reshape(v.shape[:-1] + (-1, 32))
    amax = np.abs(blocks).max(-1, keepdims=True)
    byte = np.maximum(np.where(amax > 0, np.frexp(amax)[1] - 1 + 127, 0) - down, 1)
    scale = np.exp2(byte - 127.0)
    codes = (blocks / scale).astype(np.float32).astype(dtype).astype(np.float64)
    return np.moveaxis((codes * scale).reshape(v.shape), -1, axis)


WIDE = False


def mx_kscale(k):
    if not WIDE:
        return np.ones(k)
    levels = np.array([10, -10, 5, -5, 0])
    a = np.random.permutation(np.resize(levels, k // 512 * 4)).reshape(k // 512, 4)
    idx = np.arange(k)
    return np.exp2(a[idx // 512, idx % 128 // 32])


BF16 = ml_dtypes.bfloat16


def bf(x):
    return np.asarray(x, np.float32).astype(BF16)


def f64(x):
    return np.asarray(x).astype(np.float64)


B, C, IC, H, W, OC = 1, 4096, 256, 32, 64, 256
N = H * W
TS = np.sqrt(2.0 / np.sqrt(IC))


def setup_inputs():
    s = mx_kscale(C)
    return {"x": bf(np.random.standard_normal((B, C, H, W)) * s[None, :, None, None]),
            "w_g": bf(np.random.standard_normal((IC, C)) * 2.0 / np.sqrt(C) / s[None, :]),
            "theta": bf(np.random.standard_normal((B, N, IC)) * TS),
            "phi": bf(np.random.standard_normal((B, IC, N)) * TS)}


def reference(x, w_g, theta, phi):
    xf = f64(x).reshape(B, C, N)
    g = mxq(xf, 1, "e4m3").transpose(0, 2, 1) @ mxq(f64(w_g), 1, "e4m3").T
    sc = f64(theta) @ f64(phi)
    e = np.exp(sc - sc.max(1, keepdims=True))
    attn = e / e.sum(1, keepdims=True)
    y = mxq(attn, 2, "e4m3") @ mxq(g, 1, "e4m3")
    return y.transpose(0, 2, 1).reshape(B, IC, H, W)

@@ -1,0 +1,418 @@
+from contextlib import ExitStack
+
+import concourse.masks as masks
+import concourse.mybir as mybir
+
+BF16 = mybir.dt.bfloat16
+F32 = mybir.dt.float32
+U32 = mybir.dt.uint32
+U8 = mybir.dt.uint8
+FP8X4 = mybir.dt.float8_e4m3fn_x4
+AX = mybir.AxisListType.X
+ALU = mybir.AluOpType
+ACT = mybir.ActivationFunctionType
+
+P = 128
+C = 4096
+N = 2048
+IC = 256
+FLOPS = 2 * N * IC * C + 2 * 2 * N * N * IC
+
+NT = 16
+NPAIR = [0, 1, 2, 2, 2, 1, 1, 1, 1, 1, 1, 1, 1, 0, 0, 0]
+RAW_BUFS = 6
+NAR = [0, 0, 0, 0, 1, 1, 1, 1, 1, 1, 1, 1, 1, 1, 2, 0]
+AR_ENG = ["ssss", "sssv", "ssss", "vsvs"]
+
+
+def tile_nonlocalblock_pa_kernel(tc, x, w_g, theta, phi, out):
+    nc = tc.nc
+    x2 = x.rearrange("b c h w -> (b c) (h w)")
+    th2 = theta.rearrange("b n i -> (b n) i")
+    ph2 = phi.rearrange("b i m -> (b i) m")
+    out2 = out.rearrange("b i h w -> (b i) (h w)")
+
+    with ExitStack() as ctx:
+        const = ctx.enter_context(tc.tile_pool(name="const", bufs=1))
+        raw_pool = ctx.enter_context(tc.tile_pool(name="rawp", bufs=RAW_BUFS))
+        xg_pool = ctx.enter_context(tc.tile_pool(name="xgp", bufs=4))
+        xc_pool = ctx.enter_context(tc.tile_pool(name="xcp", bufs=6))
+        e_pool = ctx.enter_context(tc.tile_pool(name="ep", bufs=2))
+        ab_pool = ctx.enter_context(tc.tile_pool(name="abp", bufs=2))
+        ag_pool = ctx.enter_context(tc.tile_pool(name="agp", bufs=2))
+        gg_pool = ctx.enter_context(tc.tile_pool(name="ggp", bufs=2))
+        st_pool = ctx.enter_context(tc.tile_pool(name="stp", bufs=3))
+        ps_s = ctx.enter_context(tc.psum_pool(name="ps_s", bufs=6))
+        ps_g = ctx.enter_context(tc.psum_pool(name="ps_g", bufs=2))
+        ctx.enter_context(tc.manual_schedule())
+
+        ident_b = const.tile([P, P], BF16, name="ident_b")
+        ident_f = const.tile([P, P], F32, name="ident_f")
+        th_t = const.tile([P, 2, N], BF16, name="th_t")
+        phi_sb = const.tile([P, 2, N], BF16, name="phi_sb")
+        wcodes = const.tile([P, 8 * IC], U32, name="wcodes", align_bytes=64)
+        wscales = const.tile([P, 8 * IC], U8, name="wscales", align_bytes=64)
+        acodes = const.tile([P, 4 * N], U32, name="acodes", align_bytes=64)
+        ascales = const.tile([P, 4 * N], U8, name="ascales", align_bytes=64)
+        gcodes = const.tile([P, 4 * IC], U32, name="gcodes", align_bytes=64)
+        gscales = const.tile([P, 4 * IC], U8, name="gscales", align_bytes=64)
+        zero1 = const.tile([P, 1], F32, name="zero1")
+        junk1 = const.tile([P, 1], F32, name="junk1")
+
+        raw = {}
+        xg = {}
+        xc = {}
+        xs = {}
+        s_ps = {}
+        e_t = {}
+        nmx_t = {}
+        sm4_t = {}
+        abf = {}
+        agrp = {}
+        wt_ps = {}
+        wgrp = {}
+        ar_queue = []
+        state = {"pair": 0, "xq": 0, "wev": 0, "ar": 0, "pv": [], "ps": [], "gm": []}
+
+        def copy_on(eng, dst, src):
+            if eng == "v":
+                nc.vector.tensor_copy(out=dst, in_=src)
+            else:
+                nc.scalar.copy(out=dst, in_=src)
+
+        def flush(key):
+            fns = state[key]
+            state[key] = []
+            for fn in fns:
+                fn()
+
+        def load_x(u):
+            if u >= 32:
+                return
+            grp, c = divmod(u, 8)
+            t = raw_pool.tile([P, 4, 512], BF16, name="xraw", tag="raw")
+            nc.sync.dma_start(
+                out=t[:],
+                in_=x2[512 * c : 512 * (c + 1), 512 * grp : 512 * (grp + 1)].rearrange(
+                    "(p j) w -> p j w", j=4
+                ),
+            )
+            raw[u] = t
+
+        def x_regroup(u, eng):
+            j, a = divmod(u, 2)
+            if a == 0:
+                xg[j] = xg_pool.tile([P, 4096], BF16, name="xg", tag="xg", align_bytes=64)
+            copy_on(
+                eng,
+                xg[j][:, 2048 * a : 2048 * (a + 1)].rearrange("p (c i t) -> p c t i", i=4, t=4),
+                raw[u][:].rearrange("p t (c i) -> p c t i", i=4),
+            )
+            load_x(u + RAW_BUFS)
+
+        def x_quant(j):
+            xc[j] = xc_pool.tile([P, 1024], U32, name="xc", tag="xc", align_bytes=64)
+            xs[j] = xc_pool.tile([P, 1024], U8, name="xs", tag="xs", align_bytes=64)
+            nc.vector.quantize_mx(out=xc[j][:].bitcast(FP8X4), scales=xs[j][:], in_=xg[j][:])
+            state["xq"] = j + 1
+            if j % 4 == 3:
+                state["gm"].append(j // 4)
+
+        def x_pair_step():
+            j = state["pair"]
+            state["pair"] = j + 1
+            x_regroup(2 * j, "v")
+            x_regroup(2 * j + 1, "s")
+
+        def w_pe(g):
+            if g >= 8:
+                return
+            wt = ps_g.tile([P, 512], F32, name="wt", tag="g")
+            for h in range(2):
+                for u in range(2):
+                    base = 2048 * h + 256 * g
+                    nc.tensor.transpose(
+                        wt[:, 128 * (2 * h + u) : 128 * (2 * h + u + 1)],
+                        w32[:, base + u : base + 256 : 2],
+                        ident_f[:],
+                    )
+            wt_ps[g] = wt
+
+        def w_quant(hf):
+            nc.vector.quantize_mx(
+                out=wcodes[:, 1024 * hf : 1024 * (hf + 1)].bitcast(FP8X4),
+                scales=wscales[:, 1024 * hf : 1024 * (hf + 1)],
+                in_=wgrp[hf][:],
+            )
+
+        def w_step(eng):
+            g = state["wev"]
+            if g >= 8 or g not in wt_ps:
+                return
+            state["wev"] = g + 1
+            hf, q = divmod(g, 4)
+            if q == 0:
+                wgrp[hf] = ag_pool.tile([P, 4096], BF16, name="wgrp", tag="agrp", align_bytes=64)
+            copy_on(
+                eng,
+                wgrp[hf][:].bitcast(F32)[:, 512 * q : 512 * (q + 1)].rearrange(
+                    "p (h i u) -> p h i u", h=2, u=2
+                ),
+                wt_ps[g][:].rearrange("p (h u i) -> p h i u", h=2, u=2),
+            )
+            w_pe(g + 2)
+            if q == 3:
+                state["pv"].append(lambda: w_quant(hf))
+
+        def s_bank(i, nb):
+            sp = ps_s.tile([P, 512], F32, name="s_ps", tag="s")
+            for kh in range(2):
+                nc.tensor.matmul(
+                    out=sp[:],
+                    lhsT=phi_sb[:, kh, 128 * i : 128 * (i + 1)],
+                    rhs=th_t[:, kh, 512 * nb : 512 * (nb + 1)],
+                    start=(kh == 0),
+                    stop=(kh == 1),
+                )
+            s_ps[(i, nb)] = sp
+
+        def p1(i):
+            mx4 = st_pool.tile([P, 4], F32, name="mx4", tag="mx4")
+            for nb in range(4):
+                nc.vector.tensor_reduce(
+                    out=mx4[:, nb : nb + 1], in_=s_ps[(i, nb)][:], axis=AX, op=ALU.max
+                )
+            nmx = st_pool.tile([P, 1], F32, name="nmx", tag="nmx")
+            nc.vector.tensor_reduce(out=nmx[:], in_=mx4[:], axis=AX, op=ALU.max, negate=True)
+            nmx_t[i] = nmx
+
+        def p2(i):
+            e = e_pool.tile([P, N], F32, name="e", tag="e")
+            sm4 = st_pool.tile([P, 4], F32, name="sm4", tag="sm4")
+            for nb in range(4):
+                nc.scalar.activation(
+                    out=e[:, 512 * nb : 512 * (nb + 1)],
+                    in_=s_ps[(i, nb)][:],
+                    func=ACT.Exp,
+                    bias=nmx_t[i][:, 0:1],
+                    scale=1.0,
+                    accum_out=sm4[:, nb : nb + 1],
+                )
+            e_t[i] = e
+            sm4_t[i] = sm4
+
+        def fin(i):
+            grp, t = divmod(i, 4)
+            sm = st_pool.tile([P, 1], F32, name="sm", tag="sm")
+            nc.vector.tensor_reduce(out=sm[:], in_=sm4_t[i][:], axis=AX, op=ALU.add)
+            rc = st_pool.tile([P, 1], F32, name="rc", tag="rc")
+            nc.vector.reciprocal(out=rc[:], in_=sm[:])
+            if t == 0:
+                abf[grp] = ab_pool.tile([P, 4, N], BF16, name="abf", tag="abf")
+            nc.vector.tensor_scalar(
+                out=abf[grp][:, t, :], in0=e_t[i][:], scalar1=rc[:, 0:1], scalar2=None, op0=ALU.mult
+            )
+            if t == 3:
+                for k in range(4):
+                    ar_queue.append((grp, k))
+
+        def a_regroup(grp, k, eng):
+            kk, a = divmod(k, 2)
+            if a == 0:
+                agrp[(grp, kk)] = ag_pool.tile(
+                    [P, 4096], BF16, name="agrp", tag="agrp", align_bytes=64
+                )
+            copy_on(
+                eng,
+                agrp[(grp, kk)][:, 2048 * a : 2048 * (a + 1)].rearrange(
+                    "p (c i t) -> p c t i", i=4, t=4
+                ),
+                abf[grp][:, :, 512 * k : 512 * (k + 1)].rearrange("p t (c i) -> p c t i", i=4),
+            )
+
+        def a_quant(grp, first, width):
+            kk = first // 1024
+            off = first - 1024 * kk
+            lo = N * grp + first
+            nc.vector.quantize_mx(
+                out=acodes[:, lo : lo + width].bitcast(FP8X4),
+                scales=ascales[:, lo : lo + width],
+                in_=agrp[(grp, kk)][:, 4 * off : 4 * (off + width)],
+            )
+
+        def g_quant(grp, gg):
+            nc.vector.quantize_mx(
+                out=gcodes[:, IC * grp : IC * (grp + 1)].bitcast(FP8X4),
+                scales=gscales[:, IC * grp : IC * (grp + 1)],
+                in_=gg[:],
+            )
+
+        def g_evac(grp, gps):
+            gg = gg_pool.tile([P, 1024], BF16, name="gg", tag="gg", align_bytes=64)
+            for h in range(2):
+                nc.scalar.copy(
+                    out=gg[:, 512 * h : 512 * (h + 1)].rearrange("p (i t) -> p i t", t=4),
+                    in_=gps[h][:].rearrange("p (t i) -> p i t", t=4),
+                )
+            state["pv"].append(lambda: g_quant(grp, gg))
+
+        def g_matmuls(grp):
+            gps = []
+            for h in range(2):
+                gp = ps_g.tile([P, 512], F32, name="gp", tag="g")
+                for t in range(4):
+                    for c in range(8):
+                        j = 4 * grp + c // 2
+                        lo = 512 * (c % 2) + 128 * t
+                        wl = IC * c + 128 * h
+                        nc.tensor.matmul_mx(
+                            out=gp[:, 128 * t : 128 * (t + 1)],
+                            lhsT=xc[j][:, lo : lo + 128].bitcast(FP8X4),
+                            lhsT_scale=xs[j][:, lo : lo + 128],
+                            rhs=wcodes[:, wl : wl + 128].bitcast(FP8X4),
+                            rhs_scale=wscales[:, wl : wl + 128],
+                            start=(c == 0),
+                            stop=(c == 7),
+                        )
+                gps.append(gp)
+            state["ps"].append(lambda: g_evac(grp, gps))
+
+        masks.make_identity(nc, ident_b[:])
+        masks.make_identity(nc, ident_f[:])
+        nc.vector.memset(zero1[:], 0.0)
+        nc.scalar.activation(out=junk1[:], in_=zero1[:], func=ACT.Exp)
+
+        theta_sb = e_pool.tile([P, 16, IC], BF16, name="theta_sb", tag="e")
+        w_sb = ab_pool.tile([P, 2 * C], BF16, name="w_sb", tag="abf")
+        w32 = w_sb[:].bitcast(F32)
+
+        def load_theta(k):
+            nc.sync.dma_start(
+                out=theta_sb[:, 4 * k : 4 * (k + 1), :],
+                in_=th2[512 * k : 512 * (k + 1), :].rearrange("(a p) i -> p a i", p=P),
+            )
+
+        load_theta(0)
+        nc.sync.dma_start(
+            out=phi_sb[:, :, 0:512], in_=ph2[:, 0:512].rearrange("(k p) m -> p k m", p=P)
+        )
+        for k in range(1, 4):
+            load_theta(k)
+        load_x(0)
+        load_x(1)
+        for h in range(2):
+            nc.sync.dma_start(out=w_sb[:, C * h : C * (h + 1)], in_=w_g[P * h : P * (h + 1), :])
+        for u in range(2, RAW_BUFS):
+            load_x(u)
+        nc.sync.dma_start(
+            out=phi_sb[:, :, 512:N], in_=ph2[:, 512:N].rearrange("(k p) m -> p k m", p=P)
+        )
+
+        for k in range(4):
+            tp = ps_s.tile([P, 1024], BF16, name="tp", tag="s")
+            for kh in range(2):
+                for a in range(4):
+                    nc.tensor.transpose(
+                        tp[:, 512 * kh + 128 * a : 512 * kh + 128 * (a + 1)],
+                        theta_sb[:, 4 * k + a, 128 * kh : 128 * (kh + 1)],
+                        ident_b[:],
+                    )
+            copy_on(
+                "v" if k % 2 == 0 else "s",
+                th_t[:, :, 512 * k : 512 * (k + 1)],
+                tp[:].rearrange("p (k n) -> p k n", k=2),
+            )
+        for nb in range(4):
+            s_bank(0, nb)
+        x_pair_step()
+
+        y_ps = {}
+
+        def y_pass(nb, h, grp):
+            nc.tensor.matmul_mx(
+                out=y_ps[(nb, h)][:],
+                lhsT=gcodes[:, IC * grp + 128 * h : IC * grp + 128 * (h + 1)].bitcast(FP8X4),
+                lhsT_scale=gscales[:, IC * grp + 128 * h : IC * grp + 128 * (h + 1)],
+                rhs=acodes[:, N * grp + 512 * nb : N * grp + 512 * (nb + 1)].bitcast(FP8X4),
+                rhs_scale=ascales[:, N * grp + 512 * nb : N * grp + 512 * (nb + 1)],
+                start=(grp == 0),
+                stop=(grp == 3),
+            )
+
+        def y_open(nb, pools):
+            for h in range(2):
+                if pools[h] == "s":
+                    yp = ps_s.tile([P, 512], F32, name="yp", tag="s")
+                else:
+                    yp = ps_g.tile([P, 512], F32, name="yp2", tag="g")
+                y_ps[(nb, h)] = yp
+            for grp in range(3):
+                for h in range(2):
+                    y_pass(nb, h, grp)
+
+        def ar_pop(n_units):
+            for rep in range(n_units):
+                if state["ar"] < len(ar_queue):
+                    grp, k = ar_queue[state["ar"]]
+                    state["ar"] = state["ar"] + 1
+                    a_regroup(grp, k, AR_ENG[grp][k])
+                    if k % 2 == 1:
+                        state["pv"].append(lambda grp=grp, k=k: a_quant(grp, 1024 * (k // 2), 1024))
+
+        for i in range(NT):
+            done_pairs = state["pair"]
+            state["pv_now"] = state["pv"]
+            state["pv"] = []
+            state["ps_now"] = state["ps"]
+            state["ps"] = []
+            p1(i)
+            p2(i)
+            flush("ps_now")
+            if i + 1 < NT:
+                for nb in range(4):
+                    s_bank(i + 1, nb)
+            w_step("s")
+            for grp in state["gm"]:
+                g_matmuls(grp)
+            state["gm"] = []
+            if i == 0:
+                w_pe(0)
+                w_pe(1)
+            if i >= 1:
+                fin(i - 1)
+            flush("pv_now")
+            if i == NT - 1:
+                y_open(0, "ss")
+                y_open(1, "gg")
+            for rep in range(NPAIR[i]):
+                x_pair_step()
+                if state["xq"] < done_pairs:
+                    x_quant(state["xq"])
+                w_step("s")
+            for j in range(state["xq"], done_pairs):
+                x_quant(j)
+            w_step("s")
+            ar_pop(NAR[i])
+            w_step("s")
+        fin(NT - 1)
+
+        flush("ps")
+        a_regroup(3, 0, "v")
+        a_regroup(3, 1, "s")
+        a_regroup(3, 2, "v")
+        a_regroup(3, 3, "s")
+        flush("pv")
+
+        y_open(2, "ss")
+        y_open(3, "ss")
+        for nb in range(4):
+            a_quant(3, 512 * nb, 512)
+            for h in range(2):
+                y_pass(nb, h, 3)
+        for nb in range(4):
+            osb = raw_pool.tile([P, 2, 512], F32, name="osb", tag="raw")
+            for h in range(2):
+                copy_on("s" if nb < 2 else "v", osb[:, h, :], y_ps[(nb, h)][:])
+                nc.sync.dma_start(
+                    out=out2[P * h : P * (h + 1), 512 * nb : 512 * (nb + 1)], in_=osb[:, h, :]
+                )

@@ -21,8 +21,12 @@ FLOPS = 2 * N * IC * C + 2 * 2 * N * N * IC
 NT = 16
 NPAIR = [0, 1, 2, 2, 2, 1, 1, 1, 1, 1, 1, 1, 1, 0, 0, 0]
 RAW_BUFS = 6
-NAR = [0, 0, 0, 0, 1, 1, 1, 1, 1, 1, 1, 1, 1, 1, 2, 0]
-AR_ENG = ["ssss", "sssv", "ssss", "vsvs"]
+AR_PLAN = {
+    5: [(0, 0, "g")], 6: [(0, 1, "g")], 7: [(0, 2, "g")], 8: [(0, 3, "g")],
+    9: [(1, 0, "g")], 10: [(1, 1, "g")], 11: [(1, 2, "g")], 12: [(1, 3, "g"), (2, 0, "s")],
+    13: [(2, 1, "g"), (2, 3, "s")], 14: [(2, 2, "g")],
+}
+XENG = ["vs", "gs", "gs", "vs", "gs", "ss", "gs", "vs", "vs", "ss", "vs", "ss", "vs", "ss", "vs", "ss"]
 
 
 def tile_nonlocalblock_pa_kernel(tc, x, w_g, theta, phi, out):
@@ -72,11 +76,16 @@ def tile_nonlocalblock_pa_kernel(tc, x, w_g, theta, phi, out):
         wt_ps = {}
         wgrp = {}
         ar_queue = []
-        state = {"pair": 0, "xq": 0, "wev": 0, "ar": 0, "pv": [], "ps": [], "gm": []}
+        state = {"pair": 0, "xq": 0, "wev": 0, "ar": 0, "pv": [], "ps": [], "gm": [], "ardone": []}
 
         def copy_on(eng, dst, src):
             if eng == "v":
                 nc.vector.tensor_copy(out=dst, in_=src)
+            elif eng == "g":
+                nc.gpsimd.tensor_scalar(
+                    out=dst, in0=src, scalar1=state["one"][:, 0:1], scalar2=0.0,
+                    op0=ALU.mult, op1=ALU.add,
+                )
             else:
                 nc.scalar.copy(out=dst, in_=src)
 
@@ -101,7 +110,7 @@ def tile_nonlocalblock_pa_kernel(tc, x, w_g, theta, phi, out):
 
         def x_regroup(u, eng):
             j, a = divmod(u, 2)
-            if a == 0:
+            if j not in xg:
                 xg[j] = xg_pool.tile([P, 4096], BF16, name="xg", tag="xg", align_bytes=64)
             copy_on(
                 eng,
@@ -121,8 +130,9 @@ def tile_nonlocalblock_pa_kernel(tc, x, w_g, theta, phi, out):
         def x_pair_step():
             j = state["pair"]
             state["pair"] = j + 1
-            x_regroup(2 * j, "v")
-            x_regroup(2 * j + 1, "s")
+            for a in range(2):
+                if XENG[j][a] != "g":
+                    x_regroup(2 * j + a, XENG[j][a])
 
         def w_pe(g):
             if g >= 8:
@@ -218,7 +228,7 @@ def tile_nonlocalblock_pa_kernel(tc, x, w_g, theta, phi, out):
 
         def a_regroup(grp, k, eng):
             kk, a = divmod(k, 2)
-            if a == 0:
+            if (grp, kk) not in agrp:
                 agrp[(grp, kk)] = ag_pool.tile(
                     [P, 4096], BF16, name="agrp", tag="agrp", align_bytes=64
                 )
@@ -350,13 +360,12 @@ def tile_nonlocalblock_pa_kernel(tc, x, w_g, theta, phi, out):
                 for h in range(2):
                     y_pass(nb, h, grp)
 
-        def ar_pop(n_units):
-            for rep in range(n_units):
-                if state["ar"] < len(ar_queue):
-                    grp, k = ar_queue[state["ar"]]
-                    state["ar"] = state["ar"] + 1
-                    a_regroup(grp, k, AR_ENG[grp][k])
-                    if k % 2 == 1:
+        def ar_do(i, engines):
+            for grp, k, eng in AR_PLAN.get(i, []):
+                if eng in engines:
+                    a_regroup(grp, k, eng)
+                    state["ardone"].append((grp, k))
+                    if (grp, k ^ 1) in state["ardone"]:
                         state["pv"].append(lambda grp=grp, k=k: a_quant(grp, 1024 * (k // 2), 1024))
 
         for i in range(NT):
@@ -365,6 +374,14 @@ def tile_nonlocalblock_pa_kernel(tc, x, w_g, theta, phi, out):
             state["pv"] = []
             state["ps_now"] = state["ps"]
             state["ps"] = []
+            one = st_pool.tile([P, 1], F32, name="one", tag="one")
+            nc.vector.memset(one[:], 1.0)
+            state["one"] = one
+            ar_do(i, "g")
+            for j in range(state["pair"], state["pair"] + NPAIR[i]):
+                for a in range(2):
+                    if XENG[j][a] == "g":
+                        x_regroup(2 * j + a, "g")
             p1(i)
             p2(i)
             flush("ps_now")
@@ -392,7 +409,7 @@ def tile_nonlocalblock_pa_kernel(tc, x, w_g, theta, phi, out):
             for j in range(state["xq"], done_pairs):
                 x_quant(j)
             w_step("s")
-            ar_pop(NAR[i])
+            ar_do(i, "sv")
             w_step("s")
         fin(NT - 1)
 

@@ -19,8 +19,12 @@ IC = 256
 FLOPS = 2 * N * IC * C + 2 * 2 * N * N * IC
 
 NT = 16
-NPAIR = [0, 1, 2, 2, 2, 1, 1, 1, 1, 1, 1, 1, 1, 0, 0, 0]
+NPAIR = [1, 1, 2, 2, 2, 2, 1, 1, 1, 1, 1, 1, 0, 0, 0, 0]
 RAW_BUFS = 6
+W0 = 0
+TSPLIT = 1024
+TAIL = [("r", 0, "v"), ("r", 2, "s"), ("q", 0), ("r", 1, "v"), ("e", 0, 0, "s"), ("e", 0, 1, "s"), ("q", 1), ("q", 2), ("r", 3, "v"), ("e", 1, 0, "s"), ("e", 1, 1, "s"), ("q", 3), ("e", 2, 0, "s"), ("e", 2, 1, "s"), ("e", 3, 0, "v"), ("e", 3, 1, "s")]
+DMA_ORDER = ["t0", "p0", "t1", "t2", "t3", "x", "x", "w", "x", "x", "x", "x", "pr"]
 AR_PLAN = {
     5: [(0, 0, "g")], 6: [(0, 1, "g")], 7: [(0, 2, "g")], 8: [(0, 3, "g")],
     9: [(1, 0, "g")], 10: [(1, 1, "g")], 11: [(1, 2, "g")], 12: [(1, 3, "g"), (2, 0, "s")],
@@ -76,7 +80,7 @@ def tile_nonlocalblock_pa_kernel(tc, x, w_g, theta, phi, out):
         wt_ps = {}
         wgrp = {}
         ar_queue = []
-        state = {"pair": 0, "xq": 0, "wev": 0, "ar": 0, "pv": [], "ps": [], "gm": [], "ardone": []}
+        state = {"pair": 0, "xq": 0, "wev": 0, "ar": 0, "pv": [], "ps": [], "gm": [], "ardone": [], "ld": 0}
 
         def copy_on(eng, dst, src):
             if eng == "v":
@@ -226,7 +230,7 @@ def tile_nonlocalblock_pa_kernel(tc, x, w_g, theta, phi, out):
                 for k in range(4):
                     ar_queue.append((grp, k))
 
-        def a_regroup(grp, k, eng):
+        def a_regroup(grp, k, eng, lo=0, hi=512):
             kk, a = divmod(k, 2)
             if (grp, kk) not in agrp:
                 agrp[(grp, kk)] = ag_pool.tile(
@@ -234,10 +238,10 @@ def tile_nonlocalblock_pa_kernel(tc, x, w_g, theta, phi, out):
                 )
             copy_on(
                 eng,
-                agrp[(grp, kk)][:, 2048 * a : 2048 * (a + 1)].rearrange(
+                agrp[(grp, kk)][:, 2048 * a + 4 * lo : 2048 * a + 4 * hi].rearrange(
                     "p (c i t) -> p c t i", i=4, t=4
                 ),
-                abf[grp][:, :, 512 * k : 512 * (k + 1)].rearrange("p t (c i) -> p c t i", i=4),
+                abf[grp][:, :, 512 * k + lo : 512 * k + hi].rearrange("p t (c i) -> p c t i", i=4),
             )
 
         def a_quant(grp, first, width):
@@ -302,23 +306,27 @@ def tile_nonlocalblock_pa_kernel(tc, x, w_g, theta, phi, out):
                 in_=th2[512 * k : 512 * (k + 1), :].rearrange("(a p) i -> p a i", p=P),
             )
 
-        load_theta(0)
-        nc.sync.dma_start(
-            out=phi_sb[:, :, 0:512], in_=ph2[:, 0:512].rearrange("(k p) m -> p k m", p=P)
-        )
-        for k in range(1, 4):
-            load_theta(k)
-        load_x(0)
-        load_x(1)
-        for h in range(2):
-            nc.sync.dma_start(out=w_sb[:, C * h : C * (h + 1)], in_=w_g[P * h : P * (h + 1), :])
-        for u in range(2, RAW_BUFS):
-            load_x(u)
-        nc.sync.dma_start(
-            out=phi_sb[:, :, 512:N], in_=ph2[:, 512:N].rearrange("(k p) m -> p k m", p=P)
-        )
+        for tok in DMA_ORDER:
+            if tok[0] == "t":
+                load_theta(int(tok[1]))
+            elif tok == "p0":
+                nc.sync.dma_start(
+                    out=phi_sb[:, :, 0:512], in_=ph2[:, 0:512].rearrange("(k p) m -> p k m", p=P)
+                )
+            elif tok == "pr":
+                nc.sync.dma_start(
+                    out=phi_sb[:, :, 512:N], in_=ph2[:, 512:N].rearrange("(k p) m -> p k m", p=P)
+                )
+            elif tok == "w":
+                for h in range(2):
+                    nc.sync.dma_start(
+                        out=w_sb[:, C * h : C * (h + 1)], in_=w_g[P * h : P * (h + 1), :]
+                    )
+            else:
+                load_x(state["ld"])
+                state["ld"] = state["ld"] + 1
 
-        for k in range(4):
+        def theta_chunk(k):
             tp = ps_s.tile([P, 1024], BF16, name="tp", tag="s")
             for kh in range(2):
                 for a in range(4):
@@ -332,9 +340,15 @@ def tile_nonlocalblock_pa_kernel(tc, x, w_g, theta, phi, out):
                 th_t[:, :, 512 * k : 512 * (k + 1)],
                 tp[:].rearrange("p (k n) -> p k n", k=2),
             )
-        for nb in range(4):
-            s_bank(0, nb)
-        x_pair_step()
+
+        theta_chunk(0)
+        theta_chunk(1)
+        s_bank(0, 0)
+        theta_chunk(2)
+        s_bank(0, 1)
+        theta_chunk(3)
+        s_bank(0, 2)
+        s_bank(0, 3)
 
         y_ps = {}
 
@@ -382,25 +396,31 @@ def tile_nonlocalblock_pa_kernel(tc, x, w_g, theta, phi, out):
                 for a in range(2):
                     if XENG[j][a] == "g":
                         x_regroup(2 * j + a, "g")
-            p1(i)
-            p2(i)
-            flush("ps_now")
-            if i + 1 < NT:
-                for nb in range(4):
-                    s_bank(i + 1, nb)
-            w_step("s")
+            if 1 <= i < NT - 1:
+                s_bank(i + 1, 0)
+                s_bank(i + 1, 1)
             for grp in state["gm"]:
                 g_matmuls(grp)
             state["gm"] = []
+            if i == NT - 1:
+                y_open(0, "ss")
+                y_open(1, "gg")
+            p1(i)
+            p2(i)
+            flush("ps_now")
             if i == 0:
+                s_bank(1, 0)
+                s_bank(1, 1)
+            if i + 1 < NT:
+                s_bank(i + 1, 2)
+                s_bank(i + 1, 3)
+            w_step("s")
+            if i == W0:
                 w_pe(0)
                 w_pe(1)
             if i >= 1:
                 fin(i - 1)
             flush("pv_now")
-            if i == NT - 1:
-                y_open(0, "ss")
-                y_open(1, "gg")
             for rep in range(NPAIR[i]):
                 x_pair_step()
                 if state["xq"] < done_pairs:
@@ -411,25 +431,41 @@ def tile_nonlocalblock_pa_kernel(tc, x, w_g, theta, phi, out):
             w_step("s")
             ar_do(i, "sv")
             w_step("s")
-        fin(NT - 1)
-
+        e15 = e_t[NT - 1]
+        sm = st_pool.tile([P, 1], F32, name="sm", tag="sm")
+        nc.vector.tensor_reduce(out=sm[:], in_=sm4_t[NT - 1][:], axis=AX, op=ALU.add)
+        rc = st_pool.tile([P, 1], F32, name="rc", tag="rc")
+        nc.vector.reciprocal(out=rc[:], in_=sm[:])
+        nc.vector.tensor_scalar(
+            out=abf[3][:, 3, 0:TSPLIT], in0=e15[:, 0:TSPLIT], scalar1=rc[:, 0:1], scalar2=None,
+            op0=ALU.mult,
+        )
+        nc.scalar.activation(
+            out=abf[3][:, 3, TSPLIT:N], in_=e15[:, TSPLIT:N], func=ACT.Copy, scale=rc[:, 0:1]
+        )
         flush("ps")
-        a_regroup(3, 0, "v")
-        a_regroup(3, 1, "s")
-        a_regroup(3, 2, "v")
-        a_regroup(3, 3, "s")
         flush("pv")
-
         y_open(2, "ss")
         y_open(3, "ss")
-        for nb in range(4):
+        osb = {}
+
+        def tail_q(nb):
             a_quant(3, 512 * nb, 512)
             for h in range(2):
                 y_pass(nb, h, 3)
-        for nb in range(4):
-            osb = raw_pool.tile([P, 2, 512], F32, name="osb", tag="raw")
-            for h in range(2):
-                copy_on("s" if nb < 2 else "v", osb[:, h, :], y_ps[(nb, h)][:])
-                nc.sync.dma_start(
-                    out=out2[P * h : P * (h + 1), 512 * nb : 512 * (nb + 1)], in_=osb[:, h, :]
-                )
+
+        def tail_e(nb, h, eng):
+            if nb not in osb:
+                osb[nb] = raw_pool.tile([P, 2, 512], F32, name="osb", tag="raw")
+            copy_on(eng, osb[nb][:, h, :], y_ps[(nb, h)][:])
+            nc.sync.dma_start(
+                out=out2[P * h : P * (h + 1), 512 * nb : 512 * (nb + 1)], in_=osb[nb][:, h, :]
+            )
+
+        for op in TAIL:
+            if op[0] == "r":
+                a_regroup(3, op[1], op[2])
+            elif op[0] == "q":
+                tail_q(op[1])
+            else:
+                tail_e(op[1], op[2], op[3])

@@ -116,11 +116,18 @@ def tile_nonlocalblock_pa_kernel(tc, x, w_g, theta, phi, out):
             j, a = divmod(u, 2)
             if j not in xg:
                 xg[j] = xg_pool.tile([P, 4096], BF16, name="xg", tag="xg", align_bytes=64)
-            copy_on(
-                eng,
-                xg[j][:, 2048 * a : 2048 * (a + 1)].rearrange("p (c i t) -> p c t i", i=4, t=4),
-                raw[u][:].rearrange("p t (c i) -> p c t i", i=4),
-            )
+            if eng == "g":
+                copy_on(
+                    eng,
+                    xg[j][:, 2048 * a : 2048 * (a + 1)].rearrange("p (w t) -> p w t", t=4),
+                    raw[u][:].rearrange("p t w -> p w t"),
+                )
+            else:
+                copy_on(
+                    eng,
+                    xg[j][:, 2048 * a : 2048 * (a + 1)].rearrange("p (c i t) -> p c t i", i=4, t=4),
+                    raw[u][:].rearrange("p t (c i) -> p c t i", i=4),
+                )
             load_x(u + RAW_BUFS)
 
         def x_quant(j):
@@ -236,13 +243,24 @@ def tile_nonlocalblock_pa_kernel(tc, x, w_g, theta, phi, out):
                 agrp[(grp, kk)] = ag_pool.tile(
                     [P, 4096], BF16, name="agrp", tag="agrp", align_bytes=64
                 )
-            copy_on(
-                eng,
-                agrp[(grp, kk)][:, 2048 * a + 4 * lo : 2048 * a + 4 * hi].rearrange(
-                    "p (c i t) -> p c t i", i=4, t=4
-                ),
-                abf[grp][:, :, 512 * k + lo : 512 * k + hi].rearrange("p t (c i) -> p c t i", i=4),
-            )
+            if eng == "g":
+                copy_on(
+                    eng,
+                    agrp[(grp, kk)][:, 2048 * a + 4 * lo : 2048 * a + 4 * hi].rearrange(
+                        "p (w t) -> p w t", t=4
+                    ),
+                    abf[grp][:, :, 512 * k + lo : 512 * k + hi].rearrange("p t w -> p w t"),
+                )
+            else:
+                copy_on(
+                    eng,
+                    agrp[(grp, kk)][:, 2048 * a + 4 * lo : 2048 * a + 4 * hi].rearrange(
+                        "p (c i t) -> p c t i", i=4, t=4
+                    ),
+                    abf[grp][:, :, 512 * k + lo : 512 * k + hi].rearrange(
+                        "p t (c i) -> p c t i", i=4
+                    ),
+                )
 
         def a_quant(grp, first, width):
             kk = first // 1024

@@ -19,9 +19,13 @@ IC = 256
 FLOPS = 2 * N * IC * C + 2 * 2 * N * N * IC
 
 NT = 16
-NPAIR = [1, 1, 2, 2, 2, 2, 1, 1, 1, 1, 1, 1, 0, 0, 0, 0]
+NPAIR = [0, 1, 2, 2, 2, 1, 1, 1, 1, 1, 1, 1, 1, 0, 0, 0]
 RAW_BUFS = 6
 W0 = 0
+XV = [256, 256, 64, 576, 64, 320, 64, 384, 384, 64, 384, 64, 256, 320, 384, 384]
+PRE_STEP = True
+HEAD_NEW = False
+PE_NEW = False
 TSPLIT = 1024
 TAIL = [("r", 0, "v"), ("r", 2, "s"), ("q", 0), ("r", 1, "v"), ("e", 0, 0, "s"), ("e", 0, 1, "s"), ("q", 1), ("q", 2), ("r", 3, "v"), ("e", 1, 0, "s"), ("e", 1, 1, "s"), ("q", 3), ("e", 2, 0, "s"), ("e", 2, 1, "s"), ("e", 3, 0, "v"), ("e", 3, 1, "s")]
 DMA_ORDER = ["t0", "p0", "t1", "t2", "t3", "x", "x", "w", "x", "x", "x", "x", "pr"]
@@ -75,6 +79,7 @@ def tile_nonlocalblock_pa_kernel(tc, x, w_g, theta, phi, out):
         e_t = {}
         nmx_t = {}
         sm4_t = {}
+        rc_t = {}
         abf = {}
         agrp = {}
         wt_ps = {}
@@ -112,7 +117,7 @@ def tile_nonlocalblock_pa_kernel(tc, x, w_g, theta, phi, out):
             )
             raw[u] = t
 
-        def x_regroup(u, eng):
+        def x_regroup(u, eng, lo=0, hi=512, last=True):
             j, a = divmod(u, 2)
             if j not in xg:
                 xg[j] = xg_pool.tile([P, 4096], BF16, name="xg", tag="xg", align_bytes=64)
@@ -125,10 +130,13 @@ def tile_nonlocalblock_pa_kernel(tc, x, w_g, theta, phi, out):
             else:
                 copy_on(
                     eng,
-                    xg[j][:, 2048 * a : 2048 * (a + 1)].rearrange("p (c i t) -> p c t i", i=4, t=4),
-                    raw[u][:].rearrange("p t (c i) -> p c t i", i=4),
+                    xg[j][:, 2048 * a + 4 * lo : 2048 * a + 4 * hi].rearrange(
+                        "p (c i t) -> p c t i", i=4, t=4
+                    ),
+                    raw[u][:, :, lo:hi].rearrange("p t (c i) -> p c t i", i=4),
                 )
-            load_x(u + RAW_BUFS)
+            if last:
+                load_x(u + RAW_BUFS)
 
         def x_quant(j):
             xc[j] = xc_pool.tile([P, 1024], U32, name="xc", tag="xc", align_bytes=64)
@@ -141,9 +149,15 @@ def tile_nonlocalblock_pa_kernel(tc, x, w_g, theta, phi, out):
         def x_pair_step():
             j = state["pair"]
             state["pair"] = j + 1
+            left = XV[j]
             for a in range(2):
                 if XENG[j][a] != "g":
-                    x_regroup(2 * j + a, XENG[j][a])
+                    cv = min(left, 512)
+                    left = left - cv
+                    if cv > 0:
+                        x_regroup(2 * j + a, "v", 0, cv, cv == 512)
+                    if cv < 512:
+                        x_regroup(2 * j + a, "s", cv, 512, True)
 
         def w_pe(g):
             if g >= 8:
@@ -203,6 +217,13 @@ def tile_nonlocalblock_pa_kernel(tc, x, w_g, theta, phi, out):
                 nc.vector.tensor_reduce(
                     out=mx4[:, nb : nb + 1], in_=s_ps[(i, nb)][:], axis=AX, op=ALU.max
                 )
+                if i >= 1 and nb == 0:
+                    sm = st_pool.tile([P, 1], F32, name="sm", tag="sm")
+                    nc.vector.tensor_reduce(out=sm[:], in_=sm4_t[i - 1][:], axis=AX, op=ALU.add)
+                if i >= 1 and nb == 1:
+                    rc = st_pool.tile([P, 1], F32, name="rc", tag="rc")
+                    nc.vector.reciprocal(out=rc[:], in_=sm[:])
+                    rc_t[i - 1] = rc
             nmx = st_pool.tile([P, 1], F32, name="nmx", tag="nmx")
             nc.vector.tensor_reduce(out=nmx[:], in_=mx4[:], axis=AX, op=ALU.max, negate=True)
             nmx_t[i] = nmx
@@ -224,10 +245,7 @@ def tile_nonlocalblock_pa_kernel(tc, x, w_g, theta, phi, out):
 
         def fin(i):
             grp, t = divmod(i, 4)
-            sm = st_pool.tile([P, 1], F32, name="sm", tag="sm")
-            nc.vector.tensor_reduce(out=sm[:], in_=sm4_t[i][:], axis=AX, op=ALU.add)
-            rc = st_pool.tile([P, 1], F32, name="rc", tag="rc")
-            nc.vector.reciprocal(out=rc[:], in_=sm[:])
+            rc = rc_t[i]
             if t == 0:
                 abf[grp] = ab_pool.tile([P, 4, N], BF16, name="abf", tag="abf")
             nc.vector.tensor_scalar(
@@ -359,14 +377,22 @@ def tile_nonlocalblock_pa_kernel(tc, x, w_g, theta, phi, out):
                 tp[:].rearrange("p (k n) -> p k n", k=2),
             )
 
-        theta_chunk(0)
-        theta_chunk(1)
-        s_bank(0, 0)
-        theta_chunk(2)
-        s_bank(0, 1)
-        theta_chunk(3)
-        s_bank(0, 2)
-        s_bank(0, 3)
+        if HEAD_NEW:
+            theta_chunk(0)
+            theta_chunk(1)
+            s_bank(0, 0)
+            theta_chunk(2)
+            s_bank(0, 1)
+            theta_chunk(3)
+            s_bank(0, 2)
+            s_bank(0, 3)
+        else:
+            for k in range(4):
+                theta_chunk(k)
+            for nb in range(4):
+                s_bank(0, nb)
+        if PRE_STEP:
+            x_pair_step()
 
         y_ps = {}
 
@@ -414,31 +440,40 @@ def tile_nonlocalblock_pa_kernel(tc, x, w_g, theta, phi, out):
                 for a in range(2):
                     if XENG[j][a] == "g":
                         x_regroup(2 * j + a, "g")
-            if 1 <= i < NT - 1:
-                s_bank(i + 1, 0)
-                s_bank(i + 1, 1)
-            for grp in state["gm"]:
-                g_matmuls(grp)
-            state["gm"] = []
-            if i == NT - 1:
-                y_open(0, "ss")
-                y_open(1, "gg")
+            if PE_NEW:
+                if 1 <= i < NT - 1:
+                    s_bank(i + 1, 0)
+                    s_bank(i + 1, 1)
+                for grp in state["gm"]:
+                    g_matmuls(grp)
+                state["gm"] = []
+                if i == NT - 1:
+                    y_open(0, "ss")
             p1(i)
             p2(i)
             flush("ps_now")
-            if i == 0:
-                s_bank(1, 0)
-                s_bank(1, 1)
+            if PE_NEW and i == NT - 1:
+                y_open(1, "gg")
             if i + 1 < NT:
+                if i == 0 or not PE_NEW:
+                    s_bank(i + 1, 0)
+                    s_bank(i + 1, 1)
                 s_bank(i + 1, 2)
                 s_bank(i + 1, 3)
             w_step("s")
+            if not PE_NEW:
+                for grp in state["gm"]:
+                    g_matmuls(grp)
+                state["gm"] = []
             if i == W0:
                 w_pe(0)
                 w_pe(1)
             if i >= 1:
                 fin(i - 1)
             flush("pv_now")
+            if i == NT - 1 and not PE_NEW:
+                y_open(0, "ss")
+                y_open(1, "gg")
             for rep in range(NPAIR[i]):
                 x_pair_step()
                 if state["xq"] < done_pairs:
@@ -458,9 +493,10 @@ def tile_nonlocalblock_pa_kernel(tc, x, w_g, theta, phi, out):
             out=abf[3][:, 3, 0:TSPLIT], in0=e15[:, 0:TSPLIT], scalar1=rc[:, 0:1], scalar2=None,
             op0=ALU.mult,
         )
-        nc.scalar.activation(
-            out=abf[3][:, 3, TSPLIT:N], in_=e15[:, TSPLIT:N], func=ACT.Copy, scale=rc[:, 0:1]
-        )
+        if TSPLIT < N:
+            nc.scalar.activation(
+                out=abf[3][:, 3, TSPLIT:N], in_=e15[:, TSPLIT:N], func=ACT.Copy, scale=rc[:, 0:1]
+            )
         flush("ps")
         flush("pv")
         y_open(2, "ss")

@@ -16,25 +16,40 @@ P = 128
 C = 4096
 N = 2048
 IC = 256
+PACK = 4
+K_PASS = P * PACK
+UNIT = 512
+BANK = 512
 FLOPS = 2 * N * IC * C + 2 * 2 * N * N * IC
 
-NT = 16
-NPAIR = [0, 1, 2, 2, 2, 1, 1, 1, 1, 1, 1, 1, 1, 0, 0, 0]
-RAW_BUFS = 6
-W0 = 0
-XV = [256, 256, 64, 576, 64, 320, 64, 384, 384, 64, 384, 64, 256, 320, 384, 384]
-PRE_STEP = True
-HEAD_NEW = False
-PE_NEW = False
-TSPLIT = 1024
-TAIL = [("r", 0, "v"), ("r", 2, "s"), ("q", 0), ("r", 1, "v"), ("e", 0, 0, "s"), ("e", 0, 1, "s"), ("q", 1), ("q", 2), ("r", 3, "v"), ("e", 1, 0, "s"), ("e", 1, 1, "s"), ("q", 3), ("e", 2, 0, "s"), ("e", 2, 1, "s"), ("e", 3, 0, "v"), ("e", 3, 1, "s")]
-DMA_ORDER = ["t0", "p0", "t1", "t2", "t3", "x", "x", "w", "x", "x", "x", "x", "pr"]
-AR_PLAN = {
-    5: [(0, 0, "g")], 6: [(0, 1, "g")], 7: [(0, 2, "g")], 8: [(0, 3, "g")],
-    9: [(1, 0, "g")], 10: [(1, 1, "g")], 11: [(1, 2, "g")], 12: [(1, 3, "g"), (2, 0, "s")],
-    13: [(2, 1, "g"), (2, 3, "s")], 14: [(2, 2, "g")],
-}
-XENG = ["vs", "gs", "gs", "vs", "gs", "ss", "gs", "vs", "vs", "ss", "vs", "ss", "vs", "ss", "vs", "ss"]
+TILES = N // P
+GROUPS = TILES // PACK
+SCORE_BANKS = N // BANK
+PASSES = C // K_PASS
+X_UNITS = GROUPS * PASSES
+PAIRS_IN_GROUP = PASSES // 2
+W_BANKS = PASSES
+W_PASSES_IN_CALL = 4
+
+X_UNITS_AHEAD = 6
+
+LAST_X_PERIOD = 12
+TWO_PAIR_PERIODS = (2, 3, 4)
+
+FIRST_A_PERIOD = 5
+
+VECTOR_ONE_IN = 4
+
+LATE_GROUP = 2
+LATE_START = PACK * LATE_GROUP + PACK
+
+LAST_TILE_VECTOR_COLUMNS = 1024
+
+
+def pairs_in_period(i):
+    if i < 1 or i > LAST_X_PERIOD:
+        return 0
+    return 2 if i in TWO_PAIR_PERIODS else 1
 
 
 def tile_nonlocalblock_pa_kernel(tc, x, w_g, theta, phi, out):
@@ -46,7 +61,7 @@ def tile_nonlocalblock_pa_kernel(tc, x, w_g, theta, phi, out):
 
     with ExitStack() as ctx:
         const = ctx.enter_context(tc.tile_pool(name="const", bufs=1))
-        raw_pool = ctx.enter_context(tc.tile_pool(name="rawp", bufs=RAW_BUFS))
+        raw_pool = ctx.enter_context(tc.tile_pool(name="rawp", bufs=X_UNITS_AHEAD))
         xg_pool = ctx.enter_context(tc.tile_pool(name="xgp", bufs=4))
         xc_pool = ctx.enter_context(tc.tile_pool(name="xcp", bufs=6))
         e_pool = ctx.enter_context(tc.tile_pool(name="ep", bufs=2))
@@ -62,464 +77,442 @@ def tile_nonlocalblock_pa_kernel(tc, x, w_g, theta, phi, out):
         ident_f = const.tile([P, P], F32, name="ident_f")
         th_t = const.tile([P, 2, N], BF16, name="th_t")
         phi_sb = const.tile([P, 2, N], BF16, name="phi_sb")
-        wcodes = const.tile([P, 8 * IC], U32, name="wcodes", align_bytes=64)
-        wscales = const.tile([P, 8 * IC], U8, name="wscales", align_bytes=64)
-        acodes = const.tile([P, 4 * N], U32, name="acodes", align_bytes=64)
-        ascales = const.tile([P, 4 * N], U8, name="ascales", align_bytes=64)
-        gcodes = const.tile([P, 4 * IC], U32, name="gcodes", align_bytes=64)
-        gscales = const.tile([P, 4 * IC], U8, name="gscales", align_bytes=64)
+        wcodes = const.tile([P, PASSES * IC], U32, name="wcodes", align_bytes=64)
+        wscales = const.tile([P, PASSES * IC], U8, name="wscales", align_bytes=64)
+        acodes = const.tile([P, GROUPS * N], U32, name="acodes", align_bytes=64)
+        ascales = const.tile([P, GROUPS * N], U8, name="ascales", align_bytes=64)
+        gcodes = const.tile([P, GROUPS * IC], U32, name="gcodes", align_bytes=64)
+        gscales = const.tile([P, GROUPS * IC], U8, name="gscales", align_bytes=64)
         zero1 = const.tile([P, 1], F32, name="zero1")
         junk1 = const.tile([P, 1], F32, name="junk1")
 
-        raw = {}
-        xg = {}
-        xc = {}
-        xs = {}
-        s_ps = {}
-        e_t = {}
-        nmx_t = {}
-        sm4_t = {}
-        rc_t = {}
-        abf = {}
-        agrp = {}
-        wt_ps = {}
-        wgrp = {}
-        ar_queue = []
-        state = {"pair": 0, "xq": 0, "wev": 0, "ar": 0, "pv": [], "ps": [], "gm": [], "ardone": [], "ld": 0}
+        x_raw = {}
+        x_grouped = {}
+        x_codes = {}
+        x_scales = {}
+        score_bank = {}
+        exp_tile = {}
+        neg_max = {}
+        bank_sums = {}
+        recip_sum = {}
+        attn_bf = {}
+        a_grouped = {}
+        a_done = set()
+        w_bank = {}
+        w_grouped = {}
+        y_bank = {}
+        out_tile = {}
+        todo = {"vector_later": [], "scalar_later": [], "groups": []}
+        count = {"pairs_regrouped": 0, "pairs_quantised": 0, "w_banks_emptied": 0}
+        gate = {}
 
-        def copy_on(eng, dst, src):
-            if eng == "v":
+        def run(instructions):
+            for write in instructions:
+                write()
+
+        def copy(engine, dst, src):
+            if engine == "vector":
                 nc.vector.tensor_copy(out=dst, in_=src)
-            elif eng == "g":
+            elif engine == "scalar":
+                nc.scalar.copy(out=dst, in_=src)
+            else:
                 nc.gpsimd.tensor_scalar(
-                    out=dst, in0=src, scalar1=state["one"][:, 0:1], scalar2=0.0,
+                    out=dst, in0=src, scalar1=gate["one"][:, 0:1], scalar2=0.0,
                     op0=ALU.mult, op1=ALU.add,
                 )
+
+        def regroup(engine, dst, src):
+            if engine == "gpsimd":
+                copy(
+                    engine, dst.rearrange("p (w t) -> p w t", t=PACK), src.rearrange("p t w -> p w t")
+                )
             else:
-                nc.scalar.copy(out=dst, in_=src)
+                copy(
+                    engine,
+                    dst.rearrange("p (r i t) -> p r t i", i=4, t=PACK),
+                    src.rearrange("p t (r i) -> p r t i", i=4),
+                )
 
-        def flush(key):
-            fns = state[key]
-            state[key] = []
-            for fn in fns:
-                fn()
-
-        def load_x(u):
-            if u >= 32:
-                return
-            grp, c = divmod(u, 8)
-            t = raw_pool.tile([P, 4, 512], BF16, name="xraw", tag="raw")
+        def load_x_unit(unit):
+            group, c = divmod(unit, PASSES)
+            loaded = raw_pool.tile([P, PACK, UNIT], BF16, name="xraw", tag="raw")
             nc.sync.dma_start(
-                out=t[:],
-                in_=x2[512 * c : 512 * (c + 1), 512 * grp : 512 * (grp + 1)].rearrange(
-                    "(p j) w -> p j w", j=4
+                out=loaded[:],
+                in_=x2[K_PASS * c : K_PASS * (c + 1), UNIT * group : UNIT * (group + 1)].rearrange(
+                    "(p j) w -> p j w", j=PACK
                 ),
             )
-            raw[u] = t
+            x_raw[unit] = loaded
 
-        def x_regroup(u, eng, lo=0, hi=512, last=True):
-            j, a = divmod(u, 2)
-            if j not in xg:
-                xg[j] = xg_pool.tile([P, 4096], BF16, name="xg", tag="xg", align_bytes=64)
-            if eng == "g":
-                copy_on(
-                    eng,
-                    xg[j][:, 2048 * a : 2048 * (a + 1)].rearrange("p (w t) -> p w t", t=4),
-                    raw[u][:].rearrange("p t w -> p w t"),
+        def regroup_x(unit, engine, first, last):
+            pair, side = divmod(unit, 2)
+            if pair not in x_grouped:
+                x_grouped[pair] = xg_pool.tile(
+                    [P, 2 * UNIT * PACK], BF16, name="xg", tag="xg", align_bytes=64
                 )
-            else:
-                copy_on(
-                    eng,
-                    xg[j][:, 2048 * a + 4 * lo : 2048 * a + 4 * hi].rearrange(
-                        "p (c i t) -> p c t i", i=4, t=4
-                    ),
-                    raw[u][:, :, lo:hi].rearrange("p t (c i) -> p c t i", i=4),
-                )
-            if last:
-                load_x(u + RAW_BUFS)
+            start = UNIT * PACK * side
+            regroup(
+                engine,
+                x_grouped[pair][:, start + PACK * first : start + PACK * last],
+                x_raw[unit][:, :, first:last],
+            )
+            if last == UNIT and unit + X_UNITS_AHEAD < X_UNITS:
+                load_x_unit(unit + X_UNITS_AHEAD)
 
-        def x_quant(j):
-            xc[j] = xc_pool.tile([P, 1024], U32, name="xc", tag="xc", align_bytes=64)
-            xs[j] = xc_pool.tile([P, 1024], U8, name="xs", tag="xs", align_bytes=64)
-            nc.vector.quantize_mx(out=xc[j][:].bitcast(FP8X4), scales=xs[j][:], in_=xg[j][:])
-            state["xq"] = j + 1
-            if j % 4 == 3:
-                state["gm"].append(j // 4)
+        def regroup_x_pair(first_side):
+            pair = count["pairs_regrouped"]
+            count["pairs_regrouped"] = pair + 1
+            split = (2 - first_side) * UNIT // VECTOR_ONE_IN
+            regroup_x(2 * pair + first_side, "vector", 0, split)
+            regroup_x(2 * pair + first_side, "scalar", split, UNIT)
+            if first_side == 0:
+                regroup_x(2 * pair + 1, "scalar", 0, UNIT)
 
-        def x_pair_step():
-            j = state["pair"]
-            state["pair"] = j + 1
-            left = XV[j]
-            for a in range(2):
-                if XENG[j][a] != "g":
-                    cv = min(left, 512)
-                    left = left - cv
-                    if cv > 0:
-                        x_regroup(2 * j + a, "v", 0, cv, cv == 512)
-                    if cv < 512:
-                        x_regroup(2 * j + a, "s", cv, 512, True)
+        def quantise_x_pair():
+            pair = count["pairs_quantised"]
+            count["pairs_quantised"] = pair + 1
+            x_codes[pair] = xc_pool.tile([P, 2 * UNIT], U32, name="xc", tag="xc", align_bytes=64)
+            x_scales[pair] = xc_pool.tile([P, 2 * UNIT], U8, name="xs", tag="xs", align_bytes=64)
+            nc.vector.quantize_mx(
+                out=x_codes[pair][:].bitcast(FP8X4), scales=x_scales[pair][:], in_=x_grouped[pair][:]
+            )
+            if pair % PAIRS_IN_GROUP == PAIRS_IN_GROUP - 1:
+                todo["groups"].append(pair // PAIRS_IN_GROUP)
 
-        def w_pe(g):
-            if g >= 8:
-                return
-            wt = ps_g.tile([P, 512], F32, name="wt", tag="g")
+        def transpose_w_pass(c):
+            bank = ps_g.tile([P, BANK], F32, name="wt", tag="g")
             for h in range(2):
                 for u in range(2):
-                    base = 2048 * h + 256 * g
+                    base = (C // 2) * h + (K_PASS // 2) * c
                     nc.tensor.transpose(
-                        wt[:, 128 * (2 * h + u) : 128 * (2 * h + u + 1)],
-                        w32[:, base + u : base + 256 : 2],
+                        bank[:, P * (2 * h + u) : P * (2 * h + u + 1)],
+                        w_f32[:, base + u : base + K_PASS // 2 : 2],
                         ident_f[:],
                     )
-            wt_ps[g] = wt
+            w_bank[c] = bank
 
-        def w_quant(hf):
+        def quantise_w(call):
+            width = W_PASSES_IN_CALL * IC
             nc.vector.quantize_mx(
-                out=wcodes[:, 1024 * hf : 1024 * (hf + 1)].bitcast(FP8X4),
-                scales=wscales[:, 1024 * hf : 1024 * (hf + 1)],
-                in_=wgrp[hf][:],
+                out=wcodes[:, width * call : width * (call + 1)].bitcast(FP8X4),
+                scales=wscales[:, width * call : width * (call + 1)],
+                in_=w_grouped[call][:],
             )
 
-        def w_step(eng):
-            g = state["wev"]
-            if g >= 8 or g not in wt_ps:
+        def empty_w_bank():
+            c = count["w_banks_emptied"]
+            if c not in w_bank:
                 return
-            state["wev"] = g + 1
-            hf, q = divmod(g, 4)
+            count["w_banks_emptied"] = c + 1
+            call, q = divmod(c, W_PASSES_IN_CALL)
             if q == 0:
-                wgrp[hf] = ag_pool.tile([P, 4096], BF16, name="wgrp", tag="agrp", align_bytes=64)
-            copy_on(
-                eng,
-                wgrp[hf][:].bitcast(F32)[:, 512 * q : 512 * (q + 1)].rearrange(
+                w_grouped[call] = ag_pool.tile(
+                    [P, W_PASSES_IN_CALL * IC * PACK], BF16, name="wgrp", tag="agrp", align_bytes=64
+                )
+            copy(
+                "scalar",
+                w_grouped[call][:].bitcast(F32)[:, 2 * IC * q : 2 * IC * (q + 1)].rearrange(
                     "p (h i u) -> p h i u", h=2, u=2
                 ),
-                wt_ps[g][:].rearrange("p (h u i) -> p h i u", h=2, u=2),
+                w_bank[c][:].rearrange("p (h u i) -> p h i u", h=2, u=2),
             )
-            w_pe(g + 2)
-            if q == 3:
-                state["pv"].append(lambda: w_quant(hf))
+            if c + 2 < W_BANKS:
+                transpose_w_pass(c + 2)
+            if q == W_PASSES_IN_CALL - 1:
+                todo["vector_later"].append(lambda: quantise_w(call))
 
-        def s_bank(i, nb):
-            sp = ps_s.tile([P, 512], F32, name="s_ps", tag="s")
+        def scores(i, bank):
+            psum = ps_s.tile([P, BANK], F32, name="s_ps", tag="s")
             for kh in range(2):
                 nc.tensor.matmul(
-                    out=sp[:],
-                    lhsT=phi_sb[:, kh, 128 * i : 128 * (i + 1)],
-                    rhs=th_t[:, kh, 512 * nb : 512 * (nb + 1)],
+                    out=psum[:],
+                    lhsT=phi_sb[:, kh, P * i : P * (i + 1)],
+                    rhs=th_t[:, kh, BANK * bank : BANK * (bank + 1)],
                     start=(kh == 0),
                     stop=(kh == 1),
                 )
-            s_ps[(i, nb)] = sp
+            score_bank[(i, bank)] = psum
 
-        def p1(i):
-            mx4 = st_pool.tile([P, 4], F32, name="mx4", tag="mx4")
-            for nb in range(4):
+        def maxima(i):
+            mx4 = st_pool.tile([P, SCORE_BANKS], F32, name="mx4", tag="mx4")
+            for bank in range(SCORE_BANKS):
                 nc.vector.tensor_reduce(
-                    out=mx4[:, nb : nb + 1], in_=s_ps[(i, nb)][:], axis=AX, op=ALU.max
+                    out=mx4[:, bank : bank + 1], in_=score_bank[(i, bank)][:], axis=AX, op=ALU.max
                 )
-                if i >= 1 and nb == 0:
+                if i >= 1 and bank == 0:
                     sm = st_pool.tile([P, 1], F32, name="sm", tag="sm")
-                    nc.vector.tensor_reduce(out=sm[:], in_=sm4_t[i - 1][:], axis=AX, op=ALU.add)
-                if i >= 1 and nb == 1:
+                    nc.vector.tensor_reduce(out=sm[:], in_=bank_sums[i - 1][:], axis=AX, op=ALU.add)
+                if i >= 1 and bank == 1:
                     rc = st_pool.tile([P, 1], F32, name="rc", tag="rc")
                     nc.vector.reciprocal(out=rc[:], in_=sm[:])
-                    rc_t[i - 1] = rc
+                    recip_sum[i - 1] = rc
             nmx = st_pool.tile([P, 1], F32, name="nmx", tag="nmx")
             nc.vector.tensor_reduce(out=nmx[:], in_=mx4[:], axis=AX, op=ALU.max, negate=True)
-            nmx_t[i] = nmx
+            neg_max[i] = nmx
 
-        def p2(i):
+        def exponentials(i):
             e = e_pool.tile([P, N], F32, name="e", tag="e")
-            sm4 = st_pool.tile([P, 4], F32, name="sm4", tag="sm4")
-            for nb in range(4):
+            sm4 = st_pool.tile([P, SCORE_BANKS], F32, name="sm4", tag="sm4")
+            for bank in range(SCORE_BANKS):
                 nc.scalar.activation(
-                    out=e[:, 512 * nb : 512 * (nb + 1)],
-                    in_=s_ps[(i, nb)][:],
+                    out=e[:, BANK * bank : BANK * (bank + 1)],
+                    in_=score_bank[(i, bank)][:],
                     func=ACT.Exp,
-                    bias=nmx_t[i][:, 0:1],
+                    bias=neg_max[i][:, 0:1],
                     scale=1.0,
-                    accum_out=sm4[:, nb : nb + 1],
+                    accum_out=sm4[:, bank : bank + 1],
                 )
-            e_t[i] = e
-            sm4_t[i] = sm4
+            exp_tile[i] = e
+            bank_sums[i] = sm4
 
-        def fin(i):
-            grp, t = divmod(i, 4)
-            rc = rc_t[i]
+        def normalise(i):
+            group, t = divmod(i, PACK)
             if t == 0:
-                abf[grp] = ab_pool.tile([P, 4, N], BF16, name="abf", tag="abf")
+                attn_bf[group] = ab_pool.tile([P, PACK, N], BF16, name="abf", tag="abf")
             nc.vector.tensor_scalar(
-                out=abf[grp][:, t, :], in0=e_t[i][:], scalar1=rc[:, 0:1], scalar2=None, op0=ALU.mult
+                out=attn_bf[group][:, t, :], in0=exp_tile[i][:], scalar1=recip_sum[i][:, 0:1],
+                scalar2=None, op0=ALU.mult,
             )
-            if t == 3:
-                for k in range(4):
-                    ar_queue.append((grp, k))
 
-        def a_regroup(grp, k, eng, lo=0, hi=512):
-            kk, a = divmod(k, 2)
-            if (grp, kk) not in agrp:
-                agrp[(grp, kk)] = ag_pool.tile(
-                    [P, 4096], BF16, name="agrp", tag="agrp", align_bytes=64
+        def regroup_a_unit(group, unit, engine):
+            half, side = divmod(unit, 2)
+            if (group, half) not in a_grouped:
+                a_grouped[(group, half)] = ag_pool.tile(
+                    [P, 2 * UNIT * PACK], BF16, name="agrp", tag="agrp", align_bytes=64
                 )
-            if eng == "g":
-                copy_on(
-                    eng,
-                    agrp[(grp, kk)][:, 2048 * a + 4 * lo : 2048 * a + 4 * hi].rearrange(
-                        "p (w t) -> p w t", t=4
-                    ),
-                    abf[grp][:, :, 512 * k + lo : 512 * k + hi].rearrange("p t w -> p w t"),
-                )
-            else:
-                copy_on(
-                    eng,
-                    agrp[(grp, kk)][:, 2048 * a + 4 * lo : 2048 * a + 4 * hi].rearrange(
-                        "p (c i t) -> p c t i", i=4, t=4
-                    ),
-                    abf[grp][:, :, 512 * k + lo : 512 * k + hi].rearrange(
-                        "p t (c i) -> p c t i", i=4
-                    ),
-                )
+            regroup(
+                engine,
+                a_grouped[(group, half)][:, UNIT * PACK * side : UNIT * PACK * (side + 1)],
+                attn_bf[group][:, :, UNIT * unit : UNIT * (unit + 1)],
+            )
 
-        def a_quant(grp, first, width):
-            kk = first // 1024
-            off = first - 1024 * kk
-            lo = N * grp + first
+        def quantise_a(group, first, width):
+            half = first // (2 * UNIT)
+            offset = first - 2 * UNIT * half
+            column = N * group + first
             nc.vector.quantize_mx(
-                out=acodes[:, lo : lo + width].bitcast(FP8X4),
-                scales=ascales[:, lo : lo + width],
-                in_=agrp[(grp, kk)][:, 4 * off : 4 * (off + width)],
+                out=acodes[:, column : column + width].bitcast(FP8X4),
+                scales=ascales[:, column : column + width],
+                in_=a_grouped[(group, half)][:, PACK * offset : PACK * (offset + width)],
             )
 
-        def g_quant(grp, gg):
+        def regroup_a_unit_in_period(group, unit, engine):
+            regroup_a_unit(group, unit, engine)
+            a_done.add((group, unit))
+            if (group, unit ^ 1) in a_done:
+                todo["vector_later"].append(
+                    lambda: quantise_a(group, 2 * UNIT * (unit // 2), 2 * UNIT)
+                )
+
+        def quantise_g(group, grouped):
             nc.vector.quantize_mx(
-                out=gcodes[:, IC * grp : IC * (grp + 1)].bitcast(FP8X4),
-                scales=gscales[:, IC * grp : IC * (grp + 1)],
-                in_=gg[:],
+                out=gcodes[:, IC * group : IC * (group + 1)].bitcast(FP8X4),
+                scales=gscales[:, IC * group : IC * (group + 1)],
+                in_=grouped[:],
             )
 
-        def g_evac(grp, gps):
-            gg = gg_pool.tile([P, 1024], BF16, name="gg", tag="gg", align_bytes=64)
+        def round_g(group, banks):
+            grouped = gg_pool.tile([P, IC * PACK], BF16, name="gg", tag="gg", align_bytes=64)
             for h in range(2):
                 nc.scalar.copy(
-                    out=gg[:, 512 * h : 512 * (h + 1)].rearrange("p (i t) -> p i t", t=4),
-                    in_=gps[h][:].rearrange("p (t i) -> p i t", t=4),
+                    out=grouped[:, P * PACK * h : P * PACK * (h + 1)].rearrange(
+                        "p (i t) -> p i t", t=PACK
+                    ),
+                    in_=banks[h][:].rearrange("p (t i) -> p i t", t=PACK),
                 )
-            state["pv"].append(lambda: g_quant(grp, gg))
+            todo["vector_later"].append(lambda: quantise_g(group, grouped))
 
-        def g_matmuls(grp):
-            gps = []
+        def g_passes(group):
+            banks = []
             for h in range(2):
-                gp = ps_g.tile([P, 512], F32, name="gp", tag="g")
-                for t in range(4):
-                    for c in range(8):
-                        j = 4 * grp + c // 2
-                        lo = 512 * (c % 2) + 128 * t
-                        wl = IC * c + 128 * h
+                bank = ps_g.tile([P, BANK], F32, name="gp", tag="g")
+                for t in range(PACK):
+                    for c in range(PASSES):
+                        pair = PAIRS_IN_GROUP * group + c // 2
+                        xcol = UNIT * (c % 2) + P * t
+                        wcol = IC * c + P * h
                         nc.tensor.matmul_mx(
-                            out=gp[:, 128 * t : 128 * (t + 1)],
-                            lhsT=xc[j][:, lo : lo + 128].bitcast(FP8X4),
-                            lhsT_scale=xs[j][:, lo : lo + 128],
-                            rhs=wcodes[:, wl : wl + 128].bitcast(FP8X4),
-                            rhs_scale=wscales[:, wl : wl + 128],
+                            out=bank[:, P * t : P * (t + 1)],
+                            lhsT=x_codes[pair][:, xcol : xcol + P].bitcast(FP8X4),
+                            lhsT_scale=x_scales[pair][:, xcol : xcol + P],
+                            rhs=wcodes[:, wcol : wcol + P].bitcast(FP8X4),
+                            rhs_scale=wscales[:, wcol : wcol + P],
                             start=(c == 0),
-                            stop=(c == 7),
+                            stop=(c == PASSES - 1),
                         )
-                gps.append(gp)
-            state["ps"].append(lambda: g_evac(grp, gps))
+                banks.append(bank)
+            todo["scalar_later"].append(lambda: round_g(group, banks))
+
+        def y_pass(chunk, h, group):
+            nc.tensor.matmul_mx(
+                out=y_bank[(chunk, h)][:],
+                lhsT=gcodes[:, IC * group + P * h : IC * group + P * (h + 1)].bitcast(FP8X4),
+                lhsT_scale=gscales[:, IC * group + P * h : IC * group + P * (h + 1)],
+                rhs=acodes[:, N * group + BANK * chunk : N * group + BANK * (chunk + 1)].bitcast(FP8X4),
+                rhs_scale=ascales[:, N * group + BANK * chunk : N * group + BANK * (chunk + 1)],
+                start=(group == 0),
+                stop=(group == GROUPS - 1),
+            )
+
+        def open_y(chunk, pool):
+            for h in range(2):
+                if pool == "scores":
+                    bank = ps_s.tile([P, BANK], F32, name="yp", tag="s")
+                else:
+                    bank = ps_g.tile([P, BANK], F32, name="yp2", tag="g")
+                y_bank[(chunk, h)] = bank
+            for group in range(GROUPS - 1):
+                for h in range(2):
+                    y_pass(chunk, h, group)
+
+        def close_y(chunk):
+            quantise_a(GROUPS - 1, UNIT * chunk, UNIT)
+            for h in range(2):
+                y_pass(chunk, h, GROUPS - 1)
+
+        def store_y(chunk, h, engine):
+            if chunk not in out_tile:
+                out_tile[chunk] = raw_pool.tile([P, 2, BANK], F32, name="osb", tag="raw")
+            copy(engine, out_tile[chunk][:, h, :], y_bank[(chunk, h)][:])
+            nc.sync.dma_start(
+                out=out2[P * h : P * (h + 1), BANK * chunk : BANK * (chunk + 1)],
+                in_=out_tile[chunk][:, h, :],
+            )
 
         masks.make_identity(nc, ident_b[:])
         masks.make_identity(nc, ident_f[:])
         nc.vector.memset(zero1[:], 0.0)
         nc.scalar.activation(out=junk1[:], in_=zero1[:], func=ACT.Exp)
 
-        theta_sb = e_pool.tile([P, 16, IC], BF16, name="theta_sb", tag="e")
+        theta_sb = e_pool.tile([P, TILES, IC], BF16, name="theta_sb", tag="e")
         w_sb = ab_pool.tile([P, 2 * C], BF16, name="w_sb", tag="abf")
-        w32 = w_sb[:].bitcast(F32)
+        w_f32 = w_sb[:].bitcast(F32)
 
-        def load_theta(k):
+        def load_theta(bank):
             nc.sync.dma_start(
-                out=theta_sb[:, 4 * k : 4 * (k + 1), :],
-                in_=th2[512 * k : 512 * (k + 1), :].rearrange("(a p) i -> p a i", p=P),
+                out=theta_sb[:, 4 * bank : 4 * (bank + 1), :],
+                in_=th2[BANK * bank : BANK * (bank + 1), :].rearrange("(a p) i -> p a i", p=P),
             )
 
-        for tok in DMA_ORDER:
-            if tok[0] == "t":
-                load_theta(int(tok[1]))
-            elif tok == "p0":
-                nc.sync.dma_start(
-                    out=phi_sb[:, :, 0:512], in_=ph2[:, 0:512].rearrange("(k p) m -> p k m", p=P)
-                )
-            elif tok == "pr":
-                nc.sync.dma_start(
-                    out=phi_sb[:, :, 512:N], in_=ph2[:, 512:N].rearrange("(k p) m -> p k m", p=P)
-                )
-            elif tok == "w":
-                for h in range(2):
-                    nc.sync.dma_start(
-                        out=w_sb[:, C * h : C * (h + 1)], in_=w_g[P * h : P * (h + 1), :]
-                    )
-            else:
-                load_x(state["ld"])
-                state["ld"] = state["ld"] + 1
+        def load_phi(first, last):
+            nc.sync.dma_start(
+                out=phi_sb[:, :, first:last],
+                in_=ph2[:, first:last].rearrange("(k p) m -> p k m", p=P),
+            )
 
-        def theta_chunk(k):
-            tp = ps_s.tile([P, 1024], BF16, name="tp", tag="s")
+        load_theta(0)
+        load_phi(0, 4 * P)
+        for bank in range(1, SCORE_BANKS):
+            load_theta(bank)
+        load_x_unit(0)
+        load_x_unit(1)
+        for h in range(2):
+            nc.sync.dma_start(out=w_sb[:, C * h : C * (h + 1)], in_=w_g[P * h : P * (h + 1), :])
+        for unit in range(2, X_UNITS_AHEAD):
+            load_x_unit(unit)
+        load_phi(4 * P, N)
+
+        for bank in range(SCORE_BANKS):
+            tp = ps_s.tile([P, 2 * BANK], BF16, name="tp", tag="s")
             for kh in range(2):
                 for a in range(4):
                     nc.tensor.transpose(
-                        tp[:, 512 * kh + 128 * a : 512 * kh + 128 * (a + 1)],
-                        theta_sb[:, 4 * k + a, 128 * kh : 128 * (kh + 1)],
+                        tp[:, BANK * kh + P * a : BANK * kh + P * (a + 1)],
+                        theta_sb[:, 4 * bank + a, P * kh : P * (kh + 1)],
                         ident_b[:],
                     )
-            copy_on(
-                "v" if k % 2 == 0 else "s",
-                th_t[:, :, 512 * k : 512 * (k + 1)],
+            copy(
+                "vector" if bank % 2 == 0 else "scalar",
+                th_t[:, :, BANK * bank : BANK * (bank + 1)],
                 tp[:].rearrange("p (k n) -> p k n", k=2),
             )
+        for bank in range(SCORE_BANKS):
+            scores(0, bank)
+        regroup_x_pair(0)
 
-        if HEAD_NEW:
-            theta_chunk(0)
-            theta_chunk(1)
-            s_bank(0, 0)
-            theta_chunk(2)
-            s_bank(0, 1)
-            theta_chunk(3)
-            s_bank(0, 2)
-            s_bank(0, 3)
-        else:
-            for k in range(4):
-                theta_chunk(k)
-            for nb in range(4):
-                s_bank(0, nb)
-        if PRE_STEP:
-            x_pair_step()
+        for i in range(TILES):
+            pairs_ready = count["pairs_regrouped"]
+            vector_now = todo["vector_later"]
+            scalar_now = todo["scalar_later"]
+            todo["vector_later"] = []
+            todo["scalar_later"] = []
 
-        y_ps = {}
-
-        def y_pass(nb, h, grp):
-            nc.tensor.matmul_mx(
-                out=y_ps[(nb, h)][:],
-                lhsT=gcodes[:, IC * grp + 128 * h : IC * grp + 128 * (h + 1)].bitcast(FP8X4),
-                lhsT_scale=gscales[:, IC * grp + 128 * h : IC * grp + 128 * (h + 1)],
-                rhs=acodes[:, N * grp + 512 * nb : N * grp + 512 * (nb + 1)].bitcast(FP8X4),
-                rhs_scale=ascales[:, N * grp + 512 * nb : N * grp + 512 * (nb + 1)],
-                start=(grp == 0),
-                stop=(grp == 3),
-            )
-
-        def y_open(nb, pools):
-            for h in range(2):
-                if pools[h] == "s":
-                    yp = ps_s.tile([P, 512], F32, name="yp", tag="s")
-                else:
-                    yp = ps_g.tile([P, 512], F32, name="yp2", tag="g")
-                y_ps[(nb, h)] = yp
-            for grp in range(3):
-                for h in range(2):
-                    y_pass(nb, h, grp)
-
-        def ar_do(i, engines):
-            for grp, k, eng in AR_PLAN.get(i, []):
-                if eng in engines:
-                    a_regroup(grp, k, eng)
-                    state["ardone"].append((grp, k))
-                    if (grp, k ^ 1) in state["ardone"]:
-                        state["pv"].append(lambda grp=grp, k=k: a_quant(grp, 1024 * (k // 2), 1024))
-
-        for i in range(NT):
-            done_pairs = state["pair"]
-            state["pv_now"] = state["pv"]
-            state["pv"] = []
-            state["ps_now"] = state["ps"]
-            state["ps"] = []
             one = st_pool.tile([P, 1], F32, name="one", tag="one")
             nc.vector.memset(one[:], 1.0)
-            state["one"] = one
-            ar_do(i, "g")
-            for j in range(state["pair"], state["pair"] + NPAIR[i]):
-                for a in range(2):
-                    if XENG[j][a] == "g":
-                        x_regroup(2 * j + a, "g")
-            if PE_NEW:
-                if 1 <= i < NT - 1:
-                    s_bank(i + 1, 0)
-                    s_bank(i + 1, 1)
-                for grp in state["gm"]:
-                    g_matmuls(grp)
-                state["gm"] = []
-                if i == NT - 1:
-                    y_open(0, "ss")
-            p1(i)
-            p2(i)
-            flush("ps_now")
-            if PE_NEW and i == NT - 1:
-                y_open(1, "gg")
-            if i + 1 < NT:
-                if i == 0 or not PE_NEW:
-                    s_bank(i + 1, 0)
-                    s_bank(i + 1, 1)
-                s_bank(i + 1, 2)
-                s_bank(i + 1, 3)
-            w_step("s")
-            if not PE_NEW:
-                for grp in state["gm"]:
-                    g_matmuls(grp)
-                state["gm"] = []
-            if i == W0:
-                w_pe(0)
-                w_pe(1)
+            gate["one"] = one
+            gpsimd_has_x = 1 <= i < FIRST_A_PERIOD
+            if gpsimd_has_x:
+                regroup_x(2 * pairs_ready, "gpsimd", 0, UNIT)
+            elif FIRST_A_PERIOD <= i < FIRST_A_PERIOD + LATE_GROUP * PACK:
+                group, unit = divmod(i - FIRST_A_PERIOD, PACK)
+                regroup_a_unit_in_period(group, unit, "gpsimd")
+            elif i in (LATE_START + 1, LATE_START + 2):
+                regroup_a_unit_in_period(LATE_GROUP, i - LATE_START, "gpsimd")
+
+            maxima(i)
+            exponentials(i)
+            run(scalar_now)
+            if i + 1 < TILES:
+                for bank in range(SCORE_BANKS):
+                    scores(i + 1, bank)
+            empty_w_bank()
+            for group in todo["groups"]:
+                g_passes(group)
+            todo["groups"] = []
+            if i == 0:
+                transpose_w_pass(0)
+                transpose_w_pass(1)
+
             if i >= 1:
-                fin(i - 1)
-            flush("pv_now")
-            if i == NT - 1 and not PE_NEW:
-                y_open(0, "ss")
-                y_open(1, "gg")
-            for rep in range(NPAIR[i]):
-                x_pair_step()
-                if state["xq"] < done_pairs:
-                    x_quant(state["xq"])
-                w_step("s")
-            for j in range(state["xq"], done_pairs):
-                x_quant(j)
-            w_step("s")
-            ar_do(i, "sv")
-            w_step("s")
-        e15 = e_t[NT - 1]
+                normalise(i - 1)
+            run(vector_now)
+            if i == TILES - 1:
+                open_y(0, "scores")
+                open_y(1, "g")
+            for rep in range(pairs_in_period(i)):
+                regroup_x_pair(1 if gpsimd_has_x and rep == 0 else 0)
+                if count["pairs_quantised"] < pairs_ready:
+                    quantise_x_pair()
+                empty_w_bank()
+            for rep in range(pairs_ready - count["pairs_quantised"]):
+                quantise_x_pair()
+            empty_w_bank()
+            if i == LATE_START:
+                regroup_a_unit_in_period(LATE_GROUP, 0, "scalar")
+            if i == LATE_START + 1:
+                regroup_a_unit_in_period(LATE_GROUP, 3, "scalar")
+            empty_w_bank()
+
+        last = TILES - 1
+        split = LAST_TILE_VECTOR_COLUMNS
         sm = st_pool.tile([P, 1], F32, name="sm", tag="sm")
-        nc.vector.tensor_reduce(out=sm[:], in_=sm4_t[NT - 1][:], axis=AX, op=ALU.add)
+        nc.vector.tensor_reduce(out=sm[:], in_=bank_sums[last][:], axis=AX, op=ALU.add)
         rc = st_pool.tile([P, 1], F32, name="rc", tag="rc")
         nc.vector.reciprocal(out=rc[:], in_=sm[:])
         nc.vector.tensor_scalar(
-            out=abf[3][:, 3, 0:TSPLIT], in0=e15[:, 0:TSPLIT], scalar1=rc[:, 0:1], scalar2=None,
-            op0=ALU.mult,
+            out=attn_bf[GROUPS - 1][:, PACK - 1, 0:split], in0=exp_tile[last][:, 0:split],
+            scalar1=rc[:, 0:1], scalar2=None, op0=ALU.mult,
         )
-        if TSPLIT < N:
-            nc.scalar.activation(
-                out=abf[3][:, 3, TSPLIT:N], in_=e15[:, TSPLIT:N], func=ACT.Copy, scale=rc[:, 0:1]
-            )
-        flush("ps")
-        flush("pv")
-        y_open(2, "ss")
-        y_open(3, "ss")
-        osb = {}
-
-        def tail_q(nb):
-            a_quant(3, 512 * nb, 512)
-            for h in range(2):
-                y_pass(nb, h, 3)
-
-        def tail_e(nb, h, eng):
-            if nb not in osb:
-                osb[nb] = raw_pool.tile([P, 2, 512], F32, name="osb", tag="raw")
-            copy_on(eng, osb[nb][:, h, :], y_ps[(nb, h)][:])
-            nc.sync.dma_start(
-                out=out2[P * h : P * (h + 1), 512 * nb : 512 * (nb + 1)], in_=osb[nb][:, h, :]
-            )
-
-        for op in TAIL:
-            if op[0] == "r":
-                a_regroup(3, op[1], op[2])
-            elif op[0] == "q":
-                tail_q(op[1])
-            else:
-                tail_e(op[1], op[2], op[3])
+        nc.scalar.activation(
+            out=attn_bf[GROUPS - 1][:, PACK - 1, split:N], in_=exp_tile[last][:, split:N],
+            func=ACT.Copy, scale=rc[:, 0:1],
+        )
+        run(todo["vector_later"])
+        open_y(2, "scores")
+        open_y(3, "scores")
+        regroup_a_unit(GROUPS - 1, 0, "vector")
+        regroup_a_unit(GROUPS - 1, 2, "scalar")
+        close_y(0)
+        regroup_a_unit(GROUPS - 1, 1, "vector")
+        store_y(0, 0, "scalar")
+        store_y(0, 1, "scalar")
+        close_y(1)
+        close_y(2)
+        regroup_a_unit(GROUPS - 1, 3, "vector")
+        store_y(1, 0, "scalar")
+        store_y(1, 1, "scalar")
+        close_y(3)
+        store_y(2, 0, "scalar")
+        store_y(2, 1, "scalar")
+        store_y(3, 0, "vector")
+        store_y(3, 1, "scalar")

@@ -87,6 +87,7 @@ def tile_nonlocalblock_pa_kernel(tc, x, w_g, theta, phi, out):
         junk1 = const.tile([P, 1], F32, name="junk1")
 
         x_raw = {}
+        x_moved = {}
         x_grouped = {}
         x_codes = {}
         x_scales = {}
@@ -159,13 +160,38 @@ def tile_nonlocalblock_pa_kernel(tc, x, w_g, theta, phi, out):
             if last == UNIT and unit + X_UNITS_AHEAD < X_UNITS:
                 load_x_unit(unit + X_UNITS_AHEAD)
 
+        def move_x_unit(unit):
+            banks = []
+            for half in range(2):
+                bank = ps_g.tile([P, 2 * BANK], BF16, name="xm", tag="g")
+                for quarter in range(2):
+                    first = UNIT // 2 * half + P * quarter
+                    nc.tensor.matmul(
+                        out=bank[:, BANK * quarter : BANK * (quarter + 1)],
+                        lhsT=ident_b[:],
+                        rhs=x_raw[unit][:, :, first : first + P].rearrange("p t w -> p w t"),
+                        start=True,
+                        stop=True,
+                    )
+                banks.append(bank)
+            x_moved[unit] = banks
+            if unit + X_UNITS_AHEAD < X_UNITS:
+                load_x_unit(unit + X_UNITS_AHEAD)
+
         def regroup_x_pair(first_side):
             pair = count["pairs_regrouped"]
             count["pairs_regrouped"] = pair + 1
             split = (2 - first_side) * UNIT // VECTOR_ONE_IN
             regroup_x(2 * pair + first_side, "vector", 0, split)
             regroup_x(2 * pair + first_side, "scalar", split, UNIT)
-            if first_side == 0:
+            if 2 * pair + 1 in x_moved:
+                for half in range(2):
+                    start = UNIT * PACK + 2 * BANK * half
+                    nc.scalar.copy(
+                        out=x_grouped[pair][:, start : start + 2 * BANK],
+                        in_=x_moved[2 * pair + 1][half][:],
+                    )
+            elif first_side == 0:
                 regroup_x(2 * pair + 1, "scalar", 0, UNIT)
 
         def quantise_x_pair():
@@ -456,6 +482,8 @@ def tile_nonlocalblock_pa_kernel(tc, x, w_g, theta, phi, out):
                 for bank in range(SCORE_BANKS):
                     scores(i + 1, bank)
             empty_w_bank()
+            if FIRST_A_PERIOD <= i <= LAST_X_PERIOD and not todo["groups"]:
+                move_x_unit(2 * pairs_ready + 1)
             for group in todo["groups"]:
                 g_passes(group)
             todo["groups"] = []

@@ -181,9 +181,12 @@ def tile_nonlocalblock_pa_kernel(tc, x, w_g, theta, phi, out):
         def regroup_x_pair(first_side):
             pair = count["pairs_regrouped"]
             count["pairs_regrouped"] = pair + 1
-            split = (2 - first_side) * UNIT // VECTOR_ONE_IN
-            regroup_x(2 * pair + first_side, "vector", 0, split)
-            regroup_x(2 * pair + first_side, "scalar", split, UNIT)
+            if 2 * pair + 1 in x_moved:
+                regroup_x(2 * pair, "scalar", 0, UNIT)
+            else:
+                split = (2 - first_side) * UNIT // VECTOR_ONE_IN
+                regroup_x(2 * pair + first_side, "vector", 0, split)
+                regroup_x(2 * pair + first_side, "scalar", split, UNIT)
             if 2 * pair + 1 in x_moved:
                 for half in range(2):
                     start = UNIT * PACK + 2 * BANK * half

@@ -145,6 +145,10 @@ def tile_nonlocalblock_pa_kernel(tc, x, w_g, theta, phi, out):
             )
             x_raw[unit] = loaded
 
+        def load_next_x(unit):
+            if unit + X_UNITS_AHEAD < X_UNITS:
+                load_x_unit(unit + X_UNITS_AHEAD)
+
         def regroup_x(unit, engine, first, last):
             pair, side = divmod(unit, 2)
             if pair not in x_grouped:
@@ -157,8 +161,8 @@ def tile_nonlocalblock_pa_kernel(tc, x, w_g, theta, phi, out):
                 x_grouped[pair][:, start + PACK * first : start + PACK * last],
                 x_raw[unit][:, :, first:last],
             )
-            if last == UNIT and unit + X_UNITS_AHEAD < X_UNITS:
-                load_x_unit(unit + X_UNITS_AHEAD)
+            if last == UNIT:
+                load_next_x(unit)
 
         def move_x_unit(unit):
             banks = []
@@ -175,14 +179,13 @@ def tile_nonlocalblock_pa_kernel(tc, x, w_g, theta, phi, out):
                     )
                 banks.append(bank)
             x_moved[unit] = banks
-            if unit + X_UNITS_AHEAD < X_UNITS:
-                load_x_unit(unit + X_UNITS_AHEAD)
 
         def regroup_x_pair(first_side):
             pair = count["pairs_regrouped"]
             count["pairs_regrouped"] = pair + 1
             if 2 * pair + 1 in x_moved:
                 regroup_x(2 * pair, "scalar", 0, UNIT)
+                load_next_x(2 * pair + 1)
             else:
                 split = (2 - first_side) * UNIT // VECTOR_ONE_IN
                 regroup_x(2 * pair + first_side, "vector", 0, split)
@@ -196,6 +199,11 @@ def tile_nonlocalblock_pa_kernel(tc, x, w_g, theta, phi, out):
                     )
             elif first_side == 0:
                 regroup_x(2 * pair + 1, "scalar", 0, UNIT)
+
+        def release_gpsimd():
+            one = st_pool.tile([P, 1], F32, name="one", tag="one")
+            nc.vector.memset(one[:], 1.0)
+            gate["one"] = one
 
         def quantise_x_pair():
             pair = count["pairs_quantised"]
@@ -268,10 +276,10 @@ def tile_nonlocalblock_pa_kernel(tc, x, w_g, theta, phi, out):
                 nc.vector.tensor_reduce(
                     out=mx4[:, bank : bank + 1], in_=score_bank[(i, bank)][:], axis=AX, op=ALU.max
                 )
-                if i >= 1 and bank == 0:
+                if i >= 1 and bank == 1:
                     sm = st_pool.tile([P, 1], F32, name="sm", tag="sm")
                     nc.vector.tensor_reduce(out=sm[:], in_=bank_sums[i - 1][:], axis=AX, op=ALU.add)
-                if i >= 1 and bank == 1:
+                if i >= 1 and bank == 3:
                     rc = st_pool.tile([P, 1], F32, name="rc", tag="rc")
                     nc.vector.reciprocal(out=rc[:], in_=sm[:])
                     recip_sum[i - 1] = rc
@@ -457,7 +465,11 @@ def tile_nonlocalblock_pa_kernel(tc, x, w_g, theta, phi, out):
             )
         for bank in range(SCORE_BANKS):
             scores(0, bank)
-        regroup_x_pair(0)
+        regroup_x(0, "vector", 0, 2 * UNIT // VECTOR_ONE_IN)
+        regroup_x(0, "scalar", 2 * UNIT // VECTOR_ONE_IN, UNIT)
+        count["pairs_regrouped"] = 1
+        release_gpsimd()
+        regroup_x(1, "gpsimd", 0, UNIT)
 
         for i in range(TILES):
             pairs_ready = count["pairs_regrouped"]
@@ -466,9 +478,6 @@ def tile_nonlocalblock_pa_kernel(tc, x, w_g, theta, phi, out):
             todo["vector_later"] = []
             todo["scalar_later"] = []
 
-            one = st_pool.tile([P, 1], F32, name="one", tag="one")
-            nc.vector.memset(one[:], 1.0)
-            gate["one"] = one
             gpsimd_has_x = 1 <= i < FIRST_A_PERIOD
             if gpsimd_has_x:
                 regroup_x(2 * pairs_ready, "gpsimd", 0, UNIT)
@@ -494,8 +503,6 @@ def tile_nonlocalblock_pa_kernel(tc, x, w_g, theta, phi, out):
                 transpose_w_pass(0)
                 transpose_w_pass(1)
 
-            if i >= 1:
-                normalise(i - 1)
             run(vector_now)
             if i == TILES - 1:
                 open_y(0, "scores")
@@ -508,6 +515,10 @@ def tile_nonlocalblock_pa_kernel(tc, x, w_g, theta, phi, out):
             for rep in range(pairs_ready - count["pairs_quantised"]):
                 quantise_x_pair()
             empty_w_bank()
+            if i + 1 < TILES:
+                release_gpsimd()
+            if i >= 1:
+                normalise(i - 1)
             if i == LATE_START:
                 regroup_a_unit_in_period(LATE_GROUP, 0, "scalar")
             if i == LATE_START + 1:

@@ -40,6 +40,8 @@ FIRST_A_PERIOD = 5
 
 VECTOR_ONE_IN = 4
 
+WARM_UP_PASSES = 16
+
 LATE_GROUP = 2
 LATE_START = PACK * LATE_GROUP + PACK
 
@@ -425,6 +427,25 @@ def tile_nonlocalblock_pa_kernel(tc, x, w_g, theta, phi, out):
         w_sb = ab_pool.tile([P, 2 * C], BF16, name="w_sb", tag="abf")
         w_f32 = w_sb[:].bitcast(F32)
 
+        warm_bf = const.tile([P, K_PASS], BF16, name="warm_bf", align_bytes=64)
+        warm_codes = const.tile([P, P], U32, name="warm_codes", align_bytes=64)
+        warm_scales = const.tile([P, P], U8, name="warm_scales", align_bytes=64)
+        nc.vector.memset(warm_bf[:], 1.0)
+        nc.vector.quantize_mx(
+            out=warm_codes[:].bitcast(FP8X4), scales=warm_scales[:], in_=warm_bf[:]
+        )
+        warm_bank = ps_g.tile([P, BANK], F32, name="warm_ps", tag="g")
+        for k in range(WARM_UP_PASSES):
+            nc.tensor.matmul_mx(
+                out=warm_bank[:, 0:P],
+                lhsT=warm_codes[:].bitcast(FP8X4),
+                lhsT_scale=warm_scales[:],
+                rhs=warm_codes[:].bitcast(FP8X4),
+                rhs_scale=warm_scales[:],
+                start=True,
+                stop=True,
+            )
+
         def load_theta(bank):
             nc.sync.dma_start(
                 out=theta_sb[:, 4 * bank : 4 * (bank + 1), :],
@@ -507,18 +528,19 @@ def tile_nonlocalblock_pa_kernel(tc, x, w_g, theta, phi, out):
             if i == TILES - 1:
                 open_y(0, "scores")
                 open_y(1, "g")
-            for rep in range(pairs_in_period(i)):
-                regroup_x_pair(1 if gpsimd_has_x and rep == 0 else 0)
-                if count["pairs_quantised"] < pairs_ready:
-                    quantise_x_pair()
-                empty_w_bank()
-            for rep in range(pairs_ready - count["pairs_quantised"]):
-                quantise_x_pair()
-            empty_w_bank()
-            if i + 1 < TILES:
-                release_gpsimd()
             if i >= 1:
                 normalise(i - 1)
+            for rep in range(pairs_in_period(i)):
+                regroup_x_pair(1 if gpsimd_has_x and rep == 0 else 0)
+                empty_w_bank()
+            pairs_to_quantise = pairs_ready - count["pairs_quantised"]
+            for rep in range(pairs_to_quantise - 1):
+                quantise_x_pair()
+            if i + 1 < TILES:
+                release_gpsimd()
+            if pairs_to_quantise > 0:
+                quantise_x_pair()
+            empty_w_bank()
             if i == LATE_START:
                 regroup_a_unit_in_period(LATE_GROUP, 0, "scalar")
             if i == LATE_START + 1:
@@ -541,10 +563,10 @@ def tile_nonlocalblock_pa_kernel(tc, x, w_g, theta, phi, out):
         )
         run(todo["vector_later"])
         open_y(2, "scores")
-        open_y(3, "scores")
         regroup_a_unit(GROUPS - 1, 0, "vector")
         regroup_a_unit(GROUPS - 1, 2, "scalar")
         close_y(0)
+        open_y(3, "scores")
         regroup_a_unit(GROUPS - 1, 1, "vector")
         store_y(0, 0, "scalar")
         store_y(0, 1, "scalar")

@@ -45,7 +45,8 @@ WARM_UP_PASSES = 16
 LATE_GROUP = 2
 LATE_START = PACK * LATE_GROUP + PACK
 
-LAST_TILE_VECTOR_COLUMNS = 1024
+FIRST_SHARED_TILE = 13
+SHARED_TILE_VECTOR_COLUMNS = 1024
 
 
 def pairs_in_period(i):
@@ -103,6 +104,7 @@ def tile_nonlocalblock_pa_kernel(tc, x, w_g, theta, phi, out):
         a_done = set()
         w_bank = {}
         w_grouped = {}
+        g_bank = {}
         y_bank = {}
         out_tile = {}
         todo = {"vector_later": [], "scalar_later": [], "groups": []}
@@ -278,7 +280,7 @@ def tile_nonlocalblock_pa_kernel(tc, x, w_g, theta, phi, out):
                 nc.vector.tensor_reduce(
                     out=mx4[:, bank : bank + 1], in_=score_bank[(i, bank)][:], axis=AX, op=ALU.max
                 )
-                if i >= 1 and bank == 1:
+                if i >= 1 and bank == 2:
                     sm = st_pool.tile([P, 1], F32, name="sm", tag="sm")
                     nc.vector.tensor_reduce(out=sm[:], in_=bank_sums[i - 1][:], axis=AX, op=ALU.add)
                 if i >= 1 and bank == 3:
@@ -308,10 +310,16 @@ def tile_nonlocalblock_pa_kernel(tc, x, w_g, theta, phi, out):
             group, t = divmod(i, PACK)
             if t == 0:
                 attn_bf[group] = ab_pool.tile([P, PACK, N], BF16, name="abf", tag="abf")
+            split = SHARED_TILE_VECTOR_COLUMNS if i >= FIRST_SHARED_TILE else N
             nc.vector.tensor_scalar(
-                out=attn_bf[group][:, t, :], in0=exp_tile[i][:], scalar1=recip_sum[i][:, 0:1],
-                scalar2=None, op0=ALU.mult,
+                out=attn_bf[group][:, t, 0:split], in0=exp_tile[i][:, 0:split],
+                scalar1=recip_sum[i][:, 0:1], scalar2=None, op0=ALU.mult,
             )
+            if split < N:
+                nc.scalar.activation(
+                    out=attn_bf[group][:, t, split:N], in_=exp_tile[i][:, split:N],
+                    func=ACT.Copy, scale=recip_sum[i][:, 0:1],
+                )
 
         def regroup_a_unit(group, unit, engine):
             half, side = divmod(unit, 2)
@@ -350,37 +358,36 @@ def tile_nonlocalblock_pa_kernel(tc, x, w_g, theta, phi, out):
                 in_=grouped[:],
             )
 
-        def round_g(group, banks):
+        def round_g(group):
             grouped = gg_pool.tile([P, IC * PACK], BF16, name="gg", tag="gg", align_bytes=64)
             for h in range(2):
                 nc.scalar.copy(
                     out=grouped[:, P * PACK * h : P * PACK * (h + 1)].rearrange(
                         "p (i t) -> p i t", t=PACK
                     ),
-                    in_=banks[h][:].rearrange("p (t i) -> p i t", t=PACK),
+                    in_=g_bank[(group, h)][:].rearrange("p (t i) -> p i t", t=PACK),
                 )
             todo["vector_later"].append(lambda: quantise_g(group, grouped))
 
-        def g_passes(group):
-            banks = []
-            for h in range(2):
-                bank = ps_g.tile([P, BANK], F32, name="gp", tag="g")
-                for t in range(PACK):
-                    for c in range(PASSES):
-                        pair = PAIRS_IN_GROUP * group + c // 2
-                        xcol = UNIT * (c % 2) + P * t
-                        wcol = IC * c + P * h
-                        nc.tensor.matmul_mx(
-                            out=bank[:, P * t : P * (t + 1)],
-                            lhsT=x_codes[pair][:, xcol : xcol + P].bitcast(FP8X4),
-                            lhsT_scale=x_scales[pair][:, xcol : xcol + P],
-                            rhs=wcodes[:, wcol : wcol + P].bitcast(FP8X4),
-                            rhs_scale=wscales[:, wcol : wcol + P],
-                            start=(c == 0),
-                            stop=(c == PASSES - 1),
-                        )
-                banks.append(bank)
-            todo["scalar_later"].append(lambda: round_g(group, banks))
+        def g_passes(group, h):
+            bank = ps_g.tile([P, BANK], F32, name="gp", tag="g")
+            for t in range(PACK):
+                for c in range(PASSES):
+                    pair = PAIRS_IN_GROUP * group + c // 2
+                    xcol = UNIT * (c % 2) + P * t
+                    wcol = IC * c + P * h
+                    nc.tensor.matmul_mx(
+                        out=bank[:, P * t : P * (t + 1)],
+                        lhsT=x_codes[pair][:, xcol : xcol + P].bitcast(FP8X4),
+                        lhsT_scale=x_scales[pair][:, xcol : xcol + P],
+                        rhs=wcodes[:, wcol : wcol + P].bitcast(FP8X4),
+                        rhs_scale=wscales[:, wcol : wcol + P],
+                        start=(c == 0),
+                        stop=(c == PASSES - 1),
+                    )
+            g_bank[(group, h)] = bank
+            if h == 1:
+                todo["scalar_later"].append(lambda: round_g(group))
 
         def y_pass(chunk, h, group):
             nc.tensor.matmul_mx(
@@ -513,12 +520,15 @@ def tile_nonlocalblock_pa_kernel(tc, x, w_g, theta, phi, out):
             run(scalar_now)
             if i + 1 < TILES:
                 for bank in range(SCORE_BANKS):
+                    if bank == 2:
+                        for group in todo["groups"]:
+                            g_passes(group, 0)
                     scores(i + 1, bank)
             empty_w_bank()
             if FIRST_A_PERIOD <= i <= LAST_X_PERIOD and not todo["groups"]:
                 move_x_unit(2 * pairs_ready + 1)
             for group in todo["groups"]:
-                g_passes(group)
+                g_passes(group, 1)
             todo["groups"] = []
             if i == 0:
                 transpose_w_pass(0)
@@ -548,19 +558,12 @@ def tile_nonlocalblock_pa_kernel(tc, x, w_g, theta, phi, out):
             empty_w_bank()
 
         last = TILES - 1
-        split = LAST_TILE_VECTOR_COLUMNS
         sm = st_pool.tile([P, 1], F32, name="sm", tag="sm")
         nc.vector.tensor_reduce(out=sm[:], in_=bank_sums[last][:], axis=AX, op=ALU.add)
         rc = st_pool.tile([P, 1], F32, name="rc", tag="rc")
         nc.vector.reciprocal(out=rc[:], in_=sm[:])
-        nc.vector.tensor_scalar(
-            out=attn_bf[GROUPS - 1][:, PACK - 1, 0:split], in0=exp_tile[last][:, 0:split],
-            scalar1=rc[:, 0:1], scalar2=None, op0=ALU.mult,
-        )
-        nc.scalar.activation(
-            out=attn_bf[GROUPS - 1][:, PACK - 1, split:N], in_=exp_tile[last][:, split:N],
-            func=ACT.Copy, scale=rc[:, 0:1],
-        )
+        recip_sum[last] = rc
+        normalise(last)
         run(todo["vector_later"])
         open_y(2, "scores")
         regroup_a_unit(GROUPS - 1, 0, "vector")

@@ -520,14 +520,15 @@ def tile_nonlocalblock_pa_kernel(tc, x, w_g, theta, phi, out):
             run(scalar_now)
             if i + 1 < TILES:
                 for bank in range(SCORE_BANKS):
-                    if bank == 2:
-                        for group in todo["groups"]:
-                            g_passes(group, 0)
+                    if bank == 2 and GROUPS - 1 in todo["groups"]:
+                        g_passes(GROUPS - 1, 0)
                     scores(i + 1, bank)
             empty_w_bank()
             if FIRST_A_PERIOD <= i <= LAST_X_PERIOD and not todo["groups"]:
                 move_x_unit(2 * pairs_ready + 1)
             for group in todo["groups"]:
+                if group < GROUPS - 1:
+                    g_passes(group, 0)
                 g_passes(group, 1)
             todo["groups"] = []
             if i == 0:

from contextlib import ExitStack

import concourse.masks as masks
import concourse.mybir as mybir

BF16 = mybir.dt.bfloat16
F32 = mybir.dt.float32
U32 = mybir.dt.uint32
U8 = mybir.dt.uint8
FP8X4 = mybir.dt.float8_e4m3fn_x4
AX = mybir.AxisListType.X
ALU = mybir.AluOpType
ACT = mybir.ActivationFunctionType

P = 128
C = 4096
N = 2048
IC = 256
PACK = 4
K_PASS = P * PACK
UNIT = 512
BANK = 512
FLOPS = 2 * N * IC * C + 2 * 2 * N * N * IC

TILES = N // P
GROUPS = TILES // PACK
SCORE_BANKS = N // BANK
PASSES = C // K_PASS
X_UNITS = GROUPS * PASSES
PAIRS_IN_GROUP = PASSES // 2
W_BANKS = PASSES
W_PASSES_IN_CALL = 4

X_UNITS_AHEAD = 6

LAST_X_PERIOD = 12
TWO_PAIR_PERIODS = (2, 3, 4)

FIRST_A_PERIOD = 5

VECTOR_ONE_IN = 4

WARM_UP_PASSES = 16

LATE_GROUP = 2
LATE_START = PACK * LATE_GROUP + PACK

FIRST_SHARED_TILE = 13
SHARED_TILE_VECTOR_COLUMNS = 1024


def pairs_in_period(i):
    if i < 1 or i > LAST_X_PERIOD:
        return 0
    return 2 if i in TWO_PAIR_PERIODS else 1


def tile_nonlocalblock_pa_kernel(tc, x, w_g, theta, phi, out):
    nc = tc.nc
    x2 = x.rearrange("b c h w -> (b c) (h w)")
    th2 = theta.rearrange("b n i -> (b n) i")
    ph2 = phi.rearrange("b i m -> (b i) m")
    out2 = out.rearrange("b i h w -> (b i) (h w)")

    with ExitStack() as ctx:
        const = ctx.enter_context(tc.tile_pool(name="const", bufs=1))
        raw_pool = ctx.enter_context(tc.tile_pool(name="rawp", bufs=X_UNITS_AHEAD))
        xg_pool = ctx.enter_context(tc.tile_pool(name="xgp", bufs=4))
        xc_pool = ctx.enter_context(tc.tile_pool(name="xcp", bufs=6))
        e_pool = ctx.enter_context(tc.tile_pool(name="ep", bufs=2))
        ab_pool = ctx.enter_context(tc.tile_pool(name="abp", bufs=2))
        ag_pool = ctx.enter_context(tc.tile_pool(name="agp", bufs=2))
        gg_pool = ctx.enter_context(tc.tile_pool(name="ggp", bufs=2))
        st_pool = ctx.enter_context(tc.tile_pool(name="stp", bufs=3))
        ps_s = ctx.enter_context(tc.psum_pool(name="ps_s", bufs=6))
        ps_g = ctx.enter_context(tc.psum_pool(name="ps_g", bufs=2))
        ctx.enter_context(tc.manual_schedule())

        ident_b = const.tile([P, P], BF16, name="ident_b")
        ident_f = const.tile([P, P], F32, name="ident_f")
        th_t = const.tile([P, 2, N], BF16, name="th_t")
        phi_sb = const.tile([P, 2, N], BF16, name="phi_sb")
        wcodes = const.tile([P, PASSES * IC], U32, name="wcodes", align_bytes=64)
        wscales = const.tile([P, PASSES * IC], U8, name="wscales", align_bytes=64)
        acodes = const.tile([P, GROUPS * N], U32, name="acodes", align_bytes=64)
        ascales = const.tile([P, GROUPS * N], U8, name="ascales", align_bytes=64)
        gcodes = const.tile([P, GROUPS * IC], U32, name="gcodes", align_bytes=64)
        gscales = const.tile([P, GROUPS * IC], U8, name="gscales", align_bytes=64)
        zero1 = const.tile([P, 1], F32, name="zero1")
        junk1 = const.tile([P, 1], F32, name="junk1")

        x_raw = {}
        x_moved = {}
        x_grouped = {}
        x_codes = {}
        x_scales = {}
        score_bank = {}
        exp_tile = {}
        neg_max = {}
        bank_sums = {}
        recip_sum = {}
        attn_bf = {}
        a_grouped = {}
        a_done = set()
        w_bank = {}
        w_grouped = {}
        g_bank = {}
        y_bank = {}
        out_tile = {}
        todo = {"vector_later": [], "scalar_later": [], "groups": []}
        count = {"pairs_regrouped": 0, "pairs_quantised": 0, "w_banks_emptied": 0}
        gate = {}

        def run(instructions):
            for write in instructions:
                write()

        def copy(engine, dst, src):
            if engine == "vector":
                nc.vector.tensor_copy(out=dst, in_=src)
            elif engine == "scalar":
                nc.scalar.copy(out=dst, in_=src)
            else:
                nc.gpsimd.tensor_scalar(
                    out=dst, in0=src, scalar1=gate["one"][:, 0:1], scalar2=0.0,
                    op0=ALU.mult, op1=ALU.add,
                )

        def regroup(engine, dst, src):
            if engine == "gpsimd":
                copy(
                    engine, dst.rearrange("p (w t) -> p w t", t=PACK), src.rearrange("p t w -> p w t")
                )
            else:
                copy(
                    engine,
                    dst.rearrange("p (r i t) -> p r t i", i=4, t=PACK),
                    src.rearrange("p t (r i) -> p r t i", i=4),
                )

        def load_x_unit(unit):
            group, c = divmod(unit, PASSES)
            loaded = raw_pool.tile([P, PACK, UNIT], BF16, name="xraw", tag="raw")
            nc.sync.dma_start(
                out=loaded[:],
                in_=x2[K_PASS * c : K_PASS * (c + 1), UNIT * group : UNIT * (group + 1)].rearrange(
                    "(p j) w -> p j w", j=PACK
                ),
            )
            x_raw[unit] = loaded

        def load_next_x(unit):
            if unit + X_UNITS_AHEAD < X_UNITS:
                load_x_unit(unit + X_UNITS_AHEAD)

        def regroup_x(unit, engine, first, last):
            pair, side = divmod(unit, 2)
            if pair not in x_grouped:
                x_grouped[pair] = xg_pool.tile(
                    [P, 2 * UNIT * PACK], BF16, name="xg", tag="xg", align_bytes=64
                )
            start = UNIT * PACK * side
            regroup(
                engine,
                x_grouped[pair][:, start + PACK * first : start + PACK * last],
                x_raw[unit][:, :, first:last],
            )
            if last == UNIT:
                load_next_x(unit)

        def move_x_unit(unit):
            banks = []
            for half in range(2):
                bank = ps_g.tile([P, 2 * BANK], BF16, name="xm", tag="g")
                for quarter in range(2):
                    first = UNIT // 2 * half + P * quarter
                    nc.tensor.matmul(
                        out=bank[:, BANK * quarter : BANK * (quarter + 1)],
                        lhsT=ident_b[:],
                        rhs=x_raw[unit][:, :, first : first + P].rearrange("p t w -> p w t"),
                        start=True,
                        stop=True,
                    )
                banks.append(bank)
            x_moved[unit] = banks

        def regroup_x_pair(first_side):
            pair = count["pairs_regrouped"]
            count["pairs_regrouped"] = pair + 1
            if 2 * pair + 1 in x_moved:
                regroup_x(2 * pair, "scalar", 0, UNIT)
                load_next_x(2 * pair + 1)
            else:
                split = (2 - first_side) * UNIT // VECTOR_ONE_IN
                regroup_x(2 * pair + first_side, "vector", 0, split)
                regroup_x(2 * pair + first_side, "scalar", split, UNIT)
            if 2 * pair + 1 in x_moved:
                for half in range(2):
                    start = UNIT * PACK + 2 * BANK * half
                    nc.scalar.copy(
                        out=x_grouped[pair][:, start : start + 2 * BANK],
                        in_=x_moved[2 * pair + 1][half][:],
                    )
            elif first_side == 0:
                regroup_x(2 * pair + 1, "scalar", 0, UNIT)

        def release_gpsimd():
            one = st_pool.tile([P, 1], F32, name="one", tag="one")
            nc.vector.memset(one[:], 1.0)
            gate["one"] = one

        def quantise_x_pair():
            pair = count["pairs_quantised"]
            count["pairs_quantised"] = pair + 1
            x_codes[pair] = xc_pool.tile([P, 2 * UNIT], U32, name="xc", tag="xc", align_bytes=64)
            x_scales[pair] = xc_pool.tile([P, 2 * UNIT], U8, name="xs", tag="xs", align_bytes=64)
            nc.vector.quantize_mx(
                out=x_codes[pair][:].bitcast(FP8X4), scales=x_scales[pair][:], in_=x_grouped[pair][:]
            )
            if pair % PAIRS_IN_GROUP == PAIRS_IN_GROUP - 1:
                todo["groups"].append(pair // PAIRS_IN_GROUP)

        def transpose_w_pass(c):
            bank = ps_g.tile([P, BANK], F32, name="wt", tag="g")
            for h in range(2):
                for u in range(2):
                    base = (C // 2) * h + (K_PASS // 2) * c
                    nc.tensor.transpose(
                        bank[:, P * (2 * h + u) : P * (2 * h + u + 1)],
                        w_f32[:, base + u : base + K_PASS // 2 : 2],
                        ident_f[:],
                    )
            w_bank[c] = bank

        def quantise_w(call):
            width = W_PASSES_IN_CALL * IC
            nc.vector.quantize_mx(
                out=wcodes[:, width * call : width * (call + 1)].bitcast(FP8X4),
                scales=wscales[:, width * call : width * (call + 1)],
                in_=w_grouped[call][:],
            )

        def empty_w_bank():
            c = count["w_banks_emptied"]
            if c not in w_bank:
                return
            count["w_banks_emptied"] = c + 1
            call, q = divmod(c, W_PASSES_IN_CALL)
            if q == 0:
                w_grouped[call] = ag_pool.tile(
                    [P, W_PASSES_IN_CALL * IC * PACK], BF16, name="wgrp", tag="agrp", align_bytes=64
                )
            copy(
                "scalar",
                w_grouped[call][:].bitcast(F32)[:, 2 * IC * q : 2 * IC * (q + 1)].rearrange(
                    "p (h i u) -> p h i u", h=2, u=2
                ),
                w_bank[c][:].rearrange("p (h u i) -> p h i u", h=2, u=2),
            )
            if c + 2 < W_BANKS:
                transpose_w_pass(c + 2)
            if q == W_PASSES_IN_CALL - 1:
                todo["vector_later"].append(lambda: quantise_w(call))

        def scores(i, bank):
            psum = ps_s.tile([P, BANK], F32, name="s_ps", tag="s")
            for kh in range(2):
                nc.tensor.matmul(
                    out=psum[:],
                    lhsT=phi_sb[:, kh, P * i : P * (i + 1)],
                    rhs=th_t[:, kh, BANK * bank : BANK * (bank + 1)],
                    start=(kh == 0),
                    stop=(kh == 1),
                )
            score_bank[(i, bank)] = psum

        def maxima(i):
            mx4 = st_pool.tile([P, SCORE_BANKS], F32, name="mx4", tag="mx4")
            for bank in range(SCORE_BANKS):
                nc.vector.tensor_reduce(
                    out=mx4[:, bank : bank + 1], in_=score_bank[(i, bank)][:], axis=AX, op=ALU.max
                )
                if i >= 1 and bank == 2:
                    sm = st_pool.tile([P, 1], F32, name="sm", tag="sm")
                    nc.vector.tensor_reduce(out=sm[:], in_=bank_sums[i - 1][:], axis=AX, op=ALU.add)
                if i >= 1 and bank == 3:
                    rc = st_pool.tile([P, 1], F32, name="rc", tag="rc")
                    nc.vector.reciprocal(out=rc[:], in_=sm[:])
                    recip_sum[i - 1] = rc
            nmx = st_pool.tile([P, 1], F32, name="nmx", tag="nmx")
            nc.vector.tensor_reduce(out=nmx[:], in_=mx4[:], axis=AX, op=ALU.max, negate=True)
            neg_max[i] = nmx

        def exponentials(i):
            e = e_pool.tile([P, N], F32, name="e", tag="e")
            sm4 = st_pool.tile([P, SCORE_BANKS], F32, name="sm4", tag="sm4")
            for bank in range(SCORE_BANKS):
                nc.scalar.activation(
                    out=e[:, BANK * bank : BANK * (bank + 1)],
                    in_=score_bank[(i, bank)][:],
                    func=ACT.Exp,
                    bias=neg_max[i][:, 0:1],
                    scale=1.0,
                    accum_out=sm4[:, bank : bank + 1],
                )
            exp_tile[i] = e
            bank_sums[i] = sm4

        def normalise(i):
            group, t = divmod(i, PACK)
            if t == 0:
                attn_bf[group] = ab_pool.tile([P, PACK, N], BF16, name="abf", tag="abf")
            split = SHARED_TILE_VECTOR_COLUMNS if i >= FIRST_SHARED_TILE else N
            nc.vector.tensor_scalar(
                out=attn_bf[group][:, t, 0:split], in0=exp_tile[i][:, 0:split],
                scalar1=recip_sum[i][:, 0:1], scalar2=None, op0=ALU.mult,
            )
            if split < N:
                nc.scalar.activation(
                    out=attn_bf[group][:, t, split:N], in_=exp_tile[i][:, split:N],
                    func=ACT.Copy, scale=recip_sum[i][:, 0:1],
                )

        def regroup_a_unit(group, unit, engine):
            half, side = divmod(unit, 2)
            if (group, half) not in a_grouped:
                a_grouped[(group, half)] = ag_pool.tile(
                    [P, 2 * UNIT * PACK], BF16, name="agrp", tag="agrp", align_bytes=64
                )
            regroup(
                engine,
                a_grouped[(group, half)][:, UNIT * PACK * side : UNIT * PACK * (side + 1)],
                attn_bf[group][:, :, UNIT * unit : UNIT * (unit + 1)],
            )

        def quantise_a(group, first, width):
            half = first // (2 * UNIT)
            offset = first - 2 * UNIT * half
            column = N * group + first
            nc.vector.quantize_mx(
                out=acodes[:, column : column + width].bitcast(FP8X4),
                scales=ascales[:, column : column + width],
                in_=a_grouped[(group, half)][:, PACK * offset : PACK * (offset + width)],
            )

        def regroup_a_unit_in_period(group, unit, engine):
            regroup_a_unit(group, unit, engine)
            a_done.add((group, unit))
            if (group, unit ^ 1) in a_done:
                todo["vector_later"].append(
                    lambda: quantise_a(group, 2 * UNIT * (unit // 2), 2 * UNIT)
                )

        def quantise_g(group, grouped):
            nc.vector.quantize_mx(
                out=gcodes[:, IC * group : IC * (group + 1)].bitcast(FP8X4),
                scales=gscales[:, IC * group : IC * (group + 1)],
                in_=grouped[:],
            )

        def round_g(group):
            grouped = gg_pool.tile([P, IC * PACK], BF16, name="gg", tag="gg", align_bytes=64)
            for h in range(2):
                nc.scalar.copy(
                    out=grouped[:, P * PACK * h : P * PACK * (h + 1)].rearrange(
                        "p (i t) -> p i t", t=PACK
                    ),
                    in_=g_bank[(group, h)][:].rearrange("p (t i) -> p i t", t=PACK),
                )
            todo["vector_later"].append(lambda: quantise_g(group, grouped))

        def g_passes(group, h):
            bank = ps_g.tile([P, BANK], F32, name="gp", tag="g")
            for t in range(PACK):
                for c in range(PASSES):
                    pair = PAIRS_IN_GROUP * group + c // 2
                    xcol = UNIT * (c % 2) + P * t
                    wcol = IC * c + P * h
                    nc.tensor.matmul_mx(
                        out=bank[:, P * t : P * (t + 1)],
                        lhsT=x_codes[pair][:, xcol : xcol + P].bitcast(FP8X4),
                        lhsT_scale=x_scales[pair][:, xcol : xcol + P],
                        rhs=wcodes[:, wcol : wcol + P].bitcast(FP8X4),
                        rhs_scale=wscales[:, wcol : wcol + P],
                        start=(c == 0),
                        stop=(c == PASSES - 1),
                    )
            g_bank[(group, h)] = bank
            if h == 1:
                todo["scalar_later"].append(lambda: round_g(group))

        def y_pass(chunk, h, group):
            nc.tensor.matmul_mx(
                out=y_bank[(chunk, h)][:],
                lhsT=gcodes[:, IC * group + P * h : IC * group + P * (h + 1)].bitcast(FP8X4),
                lhsT_scale=gscales[:, IC * group + P * h : IC * group + P * (h + 1)],
                rhs=acodes[:, N * group + BANK * chunk : N * group + BANK * (chunk + 1)].bitcast(FP8X4),
                rhs_scale=ascales[:, N * group + BANK * chunk : N * group + BANK * (chunk + 1)],
                start=(group == 0),
                stop=(group == GROUPS - 1),
            )

        def open_y(chunk, pool):
            for h in range(2):
                if pool == "scores":
                    bank = ps_s.tile([P, BANK], F32, name="yp", tag="s")
                else:
                    bank = ps_g.tile([P, BANK], F32, name="yp2", tag="g")
                y_bank[(chunk, h)] = bank
            for group in range(GROUPS - 1):
                for h in range(2):
                    y_pass(chunk, h, group)

        def close_y(chunk):
            quantise_a(GROUPS - 1, UNIT * chunk, UNIT)
            for h in range(2):
                y_pass(chunk, h, GROUPS - 1)

        def store_y(chunk, h, engine):
            if chunk not in out_tile:
                out_tile[chunk] = raw_pool.tile([P, 2, BANK], F32, name="osb", tag="raw")
            copy(engine, out_tile[chunk][:, h, :], y_bank[(chunk, h)][:])
            nc.sync.dma_start(
                out=out2[P * h : P * (h + 1), BANK * chunk : BANK * (chunk + 1)],
                in_=out_tile[chunk][:, h, :],
            )

        masks.make_identity(nc, ident_b[:])
        masks.make_identity(nc, ident_f[:])
        nc.vector.memset(zero1[:], 0.0)
        nc.scalar.activation(out=junk1[:], in_=zero1[:], func=ACT.Exp)

        theta_sb = e_pool.tile([P, TILES, IC], BF16, name="theta_sb", tag="e")
        w_sb = ab_pool.tile([P, 2 * C], BF16, name="w_sb", tag="abf")
        w_f32 = w_sb[:].bitcast(F32)

        warm_bf = const.tile([P, K_PASS], BF16, name="warm_bf", align_bytes=64)
        warm_codes = const.tile([P, P], U32, name="warm_codes", align_bytes=64)
        warm_scales = const.tile([P, P], U8, name="warm_scales", align_bytes=64)
        nc.vector.memset(warm_bf[:], 1.0)
        nc.vector.quantize_mx(
            out=warm_codes[:].bitcast(FP8X4), scales=warm_scales[:], in_=warm_bf[:]
        )
        warm_bank = ps_g.tile([P, BANK], F32, name="warm_ps", tag="g")
        for k in range(WARM_UP_PASSES):
            nc.tensor.matmul_mx(
                out=warm_bank[:, 0:P],
                lhsT=warm_codes[:].bitcast(FP8X4),
                lhsT_scale=warm_scales[:],
                rhs=warm_codes[:].bitcast(FP8X4),
                rhs_scale=warm_scales[:],
                start=True,
                stop=True,
            )

        def load_theta(bank):
            nc.sync.dma_start(
                out=theta_sb[:, 4 * bank : 4 * (bank + 1), :],
                in_=th2[BANK * bank : BANK * (bank + 1), :].rearrange("(a p) i -> p a i", p=P),
            )

        def load_phi(first, last):
            nc.sync.dma_start(
                out=phi_sb[:, :, first:last],
                in_=ph2[:, first:last].rearrange("(k p) m -> p k m", p=P),
            )

        load_theta(0)
        load_phi(0, 4 * P)
        for bank in range(1, SCORE_BANKS):
            load_theta(bank)
        load_x_unit(0)
        load_x_unit(1)
        for h in range(2):
            nc.sync.dma_start(out=w_sb[:, C * h : C * (h + 1)], in_=w_g[P * h : P * (h + 1), :])
        for unit in range(2, X_UNITS_AHEAD):
            load_x_unit(unit)
        load_phi(4 * P, N)

        for bank in range(SCORE_BANKS):
            tp = ps_s.tile([P, 2 * BANK], BF16, name="tp", tag="s")
            for kh in range(2):
                for a in range(4):
                    nc.tensor.transpose(
                        tp[:, BANK * kh + P * a : BANK * kh + P * (a + 1)],
                        theta_sb[:, 4 * bank + a, P * kh : P * (kh + 1)],
                        ident_b[:],
                    )
            copy(
                "vector" if bank % 2 == 0 else "scalar",
                th_t[:, :, BANK * bank : BANK * (bank + 1)],
                tp[:].rearrange("p (k n) -> p k n", k=2),
            )
        for bank in range(SCORE_BANKS):
            scores(0, bank)
        regroup_x(0, "vector", 0, 2 * UNIT // VECTOR_ONE_IN)
        regroup_x(0, "scalar", 2 * UNIT // VECTOR_ONE_IN, UNIT)
        count["pairs_regrouped"] = 1
        release_gpsimd()
        regroup_x(1, "gpsimd", 0, UNIT)

        for i in range(TILES):
            pairs_ready = count["pairs_regrouped"]
            vector_now = todo["vector_later"]
            scalar_now = todo["scalar_later"]
            todo["vector_later"] = []
            todo["scalar_later"] = []

            gpsimd_has_x = 1 <= i < FIRST_A_PERIOD
            if gpsimd_has_x:
                regroup_x(2 * pairs_ready, "gpsimd", 0, UNIT)
            elif FIRST_A_PERIOD <= i < FIRST_A_PERIOD + LATE_GROUP * PACK:
                group, unit = divmod(i - FIRST_A_PERIOD, PACK)
                regroup_a_unit_in_period(group, unit, "gpsimd")
            elif i in (LATE_START + 1, LATE_START + 2):
                regroup_a_unit_in_period(LATE_GROUP, i - LATE_START, "gpsimd")

            maxima(i)
            exponentials(i)
            run(scalar_now)
            if i + 1 < TILES:
                for bank in range(SCORE_BANKS):
                    if bank == 2 and GROUPS - 1 in todo["groups"]:
                        g_passes(GROUPS - 1, 0)
                    scores(i + 1, bank)
            empty_w_bank()
            if FIRST_A_PERIOD <= i <= LAST_X_PERIOD and not todo["groups"]:
                move_x_unit(2 * pairs_ready + 1)
            for group in todo["groups"]:
                if group < GROUPS - 1:
                    g_passes(group, 0)
                g_passes(group, 1)
            todo["groups"] = []
            if i == 0:
                transpose_w_pass(0)
                transpose_w_pass(1)

            run(vector_now)
            if i == TILES - 1:
                open_y(0, "scores")
                open_y(1, "g")
            if i >= 1:
                normalise(i - 1)
            for rep in range(pairs_in_period(i)):
                regroup_x_pair(1 if gpsimd_has_x and rep == 0 else 0)
                empty_w_bank()
            pairs_to_quantise = pairs_ready - count["pairs_quantised"]
            for rep in range(pairs_to_quantise - 1):
                quantise_x_pair()
            if i + 1 < TILES:
                release_gpsimd()
            if pairs_to_quantise > 0:
                quantise_x_pair()
            empty_w_bank()
            if i == LATE_START:
                regroup_a_unit_in_period(LATE_GROUP, 0, "scalar")
            if i == LATE_START + 1:
                regroup_a_unit_in_period(LATE_GROUP, 3, "scalar")
            empty_w_bank()

        last = TILES - 1
        sm = st_pool.tile([P, 1], F32, name="sm", tag="sm")
        nc.vector.tensor_reduce(out=sm[:], in_=bank_sums[last][:], axis=AX, op=ALU.add)
        rc = st_pool.tile([P, 1], F32, name="rc", tag="rc")
        nc.vector.reciprocal(out=rc[:], in_=sm[:])
        recip_sum[last] = rc
        normalise(last)
        run(todo["vector_later"])
        open_y(2, "scores")
        regroup_a_unit(GROUPS - 1, 0, "vector")
        regroup_a_unit(GROUPS - 1, 2, "scalar")
        close_y(0)
        open_y(3, "scores")
        regroup_a_unit(GROUPS - 1, 1, "vector")
        store_y(0, 0, "scalar")
        store_y(0, 1, "scalar")
        close_y(1)
        close_y(2)
        regroup_a_unit(GROUPS - 1, 3, "vector")
        store_y(1, 0, "scalar")
        store_y(1, 1, "scalar")
        close_y(3)
        store_y(2, 0, "scalar")
        store_y(2, 1, "scalar")
        store_y(3, 0, "vector")
        store_y(3, 1, "scalar")
